import numpy as np
import ml_dtypes


def mxq(x, axis, fmt="e4m3"):
    dtype, down = {"e4m3": (ml_dtypes.float8_e4m3fn, 7), "e5m2": (ml_dtypes.float8_e5m2, 14)}[fmt]
    v = np.moveaxis(np.asarray(x, np.float32).astype(ml_dtypes.bfloat16).astype(np.float64), axis, -1)
    blocks = v.reshape(v.shape[:-1] + (-1, 32))
    amax = np.abs(blocks).max(-1, keepdims=True)
    byte = np.maximum(np.where(amax > 0, np.frexp(amax)[1] - 1 + 127, 0) - down, 1)
    scale = np.exp2(byte - 127.0)
    codes = (blocks / scale).astype(np.float32).astype(dtype).astype(np.float64)
    return np.moveaxis((codes * scale).reshape(v.shape), -1, axis)


WIDE = False


def mx_kscale(k):
    if not WIDE:
        return np.ones(k)
    levels = np.array([10, -10, 5, -5, 0])
    a = np.random.permutation(np.resize(levels, k // 512 * 4)).reshape(k // 512, 4)
    idx = np.arange(k)
    return np.exp2(a[idx // 512, idx % 128 // 32])


BF16 = ml_dtypes.bfloat16


def bf(x):
    return np.asarray(x, np.float32).astype(BF16)


def f64(x):
    return np.asarray(x).astype(np.float64)


S, B, H, NC, DC = 512, 16, 512, 8, 64
ROUTINGS = 4


def squash(x, axis=-1):
    s = np.sum(x * x, axis=axis, keepdims=True)
    return x / np.sqrt(s + 1e-7)


def softmax(v, axis):
    e = np.exp(v - v.max(axis=axis, keepdims=True))
    return e / e.sum(axis=axis, keepdims=True)


def setup_inputs():
    s = mx_kscale(H)
    std = np.sqrt(2.0 / (H + NC * DC))
    return {"inputs": bf(np.random.standard_normal((S, B, H)) * s),
            "W": bf(np.random.standard_normal((1, H, NC * DC)) * std / s[None, :, None])}


def reference(inputs, W):
    x = np.transpose(f64(inputs), (1, 0, 2))
    u = mxq(x, 2, "e4m3") @ mxq(f64(W)[0], 0, "e4m3")
    u = u.reshape(B, S, NC, DC)
    u = np.transpose(u, (0, 2, 1, 3))
    b = np.zeros((B, NC, S, 1))
    outputs = None
    for i in range(ROUTINGS):
        c = softmax(b, 1)
        outputs = squash(np.sum(c * u, axis=2))
        if i < ROUTINGS - 1:
            update = np.sum(outputs[:, :, None, :] * u, axis=-1, keepdims=True)
            b = b + update
    return outputs

@@ -1,0 +1,236 @@
+from contextlib import ExitStack
+
+import concourse.masks as masks
+import concourse.mybir as mybir
+
+F32 = mybir.dt.float32
+BF16 = mybir.dt.bfloat16
+U32 = mybir.dt.uint32
+U8 = mybir.dt.uint8
+FP8X4 = mybir.dt.float8_e4m3fn_x4
+ALU = mybir.AluOpType
+ACT = mybir.ActivationFunctionType
+AX = mybir.AxisListType
+
+S, B, H, NCAP, DC = 512, 16, 512, 8, 64
+ROUNDS = 4
+P = 128
+SJ = S // P
+CG = NCAP * DC // P
+GB = 2
+NGROUPS = B // GB
+C4 = GB * CG
+EPS = 1e-7
+
+FLOPS = 2 * S * B * H * NCAP * DC + (2 * ROUNDS - 1) * 2 * S * B * NCAP * DC
+
+
+def tile_capsule_t_kernel(tc, inputs, W, out):
+    nc = tc.nc
+    with ExitStack() as ctx:
+        const = ctx.enter_context(tc.tile_pool(name="const", bufs=1))
+        xpool = ctx.enter_context(tc.tile_pool(name="xpool", bufs=2))
+        gpool = ctx.enter_context(tc.tile_pool(name="gpool", bufs=2))
+        qpool = ctx.enter_context(tc.tile_pool(name="qpool", bufs=3))
+        upool = ctx.enter_context(tc.tile_pool(name="upool", bufs=4))
+        small = ctx.enter_context(tc.tile_pool(name="small", bufs=6))
+        psum_x = ctx.enter_context(tc.psum_pool(name="psum_x", bufs=2))
+        psum_mx = ctx.enter_context(tc.psum_pool(name="psum_mx", bufs=3))
+        psum_rt = ctx.enter_context(tc.psum_pool(name="psum_rt", bufs=3))
+
+        ident = const.tile([P, P], F32, name="ident")
+        masks.make_identity(nc, ident[:])
+        blk = const.tile([P, P], F32, name="blk")
+        nc.vector.memset(blk[:], 0.0)
+        nc.vector.memset(blk[0:64, 0:64], 1.0)
+        nc.vector.memset(blk[64:128, 64:128], 1.0)
+        mask = const.tile([P, 2], F32, name="mask")
+        nc.vector.memset(mask[:], 0.0)
+        nc.vector.memset(mask[0:64, 0:1], 1.0)
+        nc.vector.memset(mask[64:128, 1:2], 1.0)
+        neghalf = const.tile([P, C4], F32, name="neghalf")
+        nc.vector.memset(neghalf[:], -0.5)
+        ofin = const.tile([P, P], F32, name="ofin")
+        nc.vector.memset(ofin[:], 0.0)
+
+        wraw = const.tile([P, 4, NCAP * DC], BF16, name="wraw")
+        nc.sync.dma_start(
+            out=wraw[:].rearrange("p (u e) c -> p u e c", u=2),
+            in_=W[0].rearrange("(u p e) c -> p u e c", u=2, e=2),
+        )
+        wg = const.tile([P, NCAP * DC, 4], BF16, name="wg", align_bytes=64)
+        nc.vector.tensor_copy(out=wg[:], in_=wraw[:].rearrange("p t c -> p c t"))
+        wq = const.tile([P, NCAP * DC], U32, name="wq", align_bytes=64)
+        ws = const.tile([P, NCAP * DC], U8, name="ws", align_bytes=64)
+        nc.vector.quantize_mx(
+            out=wq[:].bitcast(FP8X4), scales=ws[:], in_=wg[:].rearrange("p c t -> p (c t)")
+        )
+
+        xin = inputs.rearrange("(j p) b h -> p j b h", p=P)
+
+        def project(q):
+            b0 = q * GB
+            x = xpool.tile([P, SJ, GB, H], BF16, name="x")
+            nc.sync.dma_start(out=x[:], in_=xin[:, :, b0 : b0 + GB, :])
+            x32 = x[:].bitcast(F32)
+            u = upool.tile([P, GB, 2, 4, 512], F32, name="u")
+            v0 = small.tile([P, C4], F32, name="v0")
+            for bl in range(GB):
+                grouped = gpool.tile([P, 4 * S], BF16, name="grouped", align_bytes=64)
+                g32 = grouped[:].bitcast(F32)
+                for half in range(2):
+                    xt = psum_x.tile([P, 2, 2, P], F32, name="xt", tag="xt")
+                    for jj in range(2):
+                        for uu in range(2):
+                            nc.tensor.transpose(
+                                xt[:, jj, uu, :],
+                                x32[:, 2 * half + jj, bl, P * uu : P * uu + P],
+                                ident[:],
+                            )
+                    nc.scalar.copy(
+                        out=g32[:, 512 * half : 512 * half + 512].rearrange(
+                            "p (jj s uu) -> p jj s uu", jj=2, uu=2
+                        ),
+                        in_=xt[:].rearrange("p jj uu s -> p jj s uu"),
+                    )
+                xq = qpool.tile([P, S], U32, name="xq", align_bytes=64)
+                xs = qpool.tile([P, S], U8, name="xs", align_bytes=64)
+                nc.vector.quantize_mx(out=xq[:].bitcast(FP8X4), scales=xs[:], in_=grouped[:])
+                for j in range(SJ):
+                    pa = psum_mx.tile([P, 512], F32, name="pa", tag="mx")
+                    nc.tensor.matmul_mx(
+                        out=pa[:],
+                        lhsT=xq[:, P * j : P * j + P].bitcast(FP8X4),
+                        lhsT_scale=xs[:, P * j : P * j + P],
+                        rhs=wq[:].bitcast(FP8X4),
+                        rhs_scale=ws[:],
+                        start=True,
+                        stop=True,
+                    )
+                    nc.vector.tensor_copy(out=u[:, bl, 0, j, :], in_=pa[:])
+                for g in range(CG):
+                    pb = psum_mx.tile([P, 512], F32, name="pb", tag="mx")
+                    nc.tensor.matmul_mx(
+                        out=pb[:],
+                        lhsT=wq[:, P * g : P * g + P].bitcast(FP8X4),
+                        lhsT_scale=ws[:, P * g : P * g + P],
+                        rhs=xq[:].bitcast(FP8X4),
+                        rhs_scale=xs[:],
+                        start=True,
+                        stop=True,
+                    )
+                    col = bl * CG + g
+                    nc.scalar.activation(
+                        out=u[:, bl, 1, g, :],
+                        in_=pb[:],
+                        func=ACT.Copy,
+                        accum_out=v0[:, col : col + 1],
+                    )
+            return u, v0
+
+        def squash(v):
+            sq = small.tile([P, C4], F32, name="sq")
+            nc.vector.tensor_tensor(out=sq[:], in0=v[:], in1=v[:], op=ALU.mult)
+            s_ps = psum_rt.tile([P, C4], F32, name="s_ps", tag="rt")
+            nc.tensor.matmul(out=s_ps[:], lhsT=blk[:], rhs=sq[:], start=True, stop=True)
+            xe = small.tile([P, C4], F32, name="xe")
+            nc.vector.tensor_scalar(
+                out=xe[:], in0=s_ps[:], scalar1=EPS, scalar2=None, op0=ALU.add
+            )
+            rs = small.tile([P, C4], F32, name="rs")
+            nc.gpsimd.tensor_tensor(out=rs[:], in0=xe[:], in1=neghalf[:], op=ALU.pow)
+            return rs
+
+        def route(q, u, v0):
+            oblk = small.tile([P, C4, 2], F32, name="oblk")
+            v = small.tile([P, C4], F32, name="v")
+            nc.vector.tensor_scalar(
+                out=v[:], in0=v0[:], scalar1=1.0 / NCAP, scalar2=None, op0=ALU.mult
+            )
+            for r in range(ROUNDS):
+                rs = squash(v)
+                if r == ROUNDS - 1:
+                    nc.vector.tensor_tensor(
+                        out=ofin[:, q * C4 : (q + 1) * C4], in0=v[:], in1=rs[:], op=ALU.mult
+                    )
+                    break
+                o = small.tile([P, C4], F32, name="o")
+                nc.vector.tensor_tensor(out=o[:], in0=v[:], in1=rs[:], op=ALU.mult)
+                for n2 in range(2):
+                    if r == 0:
+                        nc.vector.tensor_scalar(
+                            out=oblk[:, :, n2],
+                            in0=o[:],
+                            scalar1=mask[:, n2 : n2 + 1],
+                            scalar2=None,
+                            op0=ALU.mult,
+                        )
+                    else:
+                        nc.vector.scalar_tensor_tensor(
+                            out=oblk[:, :, n2],
+                            in0=o[:],
+                            scalar=mask[:, n2 : n2 + 1],
+                            in1=oblk[:, :, n2],
+                            op0=ALU.mult,
+                            op1=ALU.add,
+                        )
+                t_ps = psum_rt.tile([P, GB * SJ, NCAP], F32, name="t_ps", tag="rt")
+                for bl in range(GB):
+                    for j in range(SJ):
+                        for g in range(CG):
+                            nc.tensor.matmul(
+                                out=t_ps[:, bl * SJ + j, 2 * g : 2 * g + 2],
+                                lhsT=u[:, bl, 1, g, P * j : P * j + P],
+                                rhs=oblk[:, bl * CG + g, :],
+                                start=True,
+                                stop=True,
+                            )
+                a = GB * SJ
+                mx = small.tile([P, a], F32, name="mx")
+                nc.vector.tensor_reduce(out=mx[:], in_=t_ps[:], axis=AX.X, op=ALU.max)
+                tm = small.tile([P, a, NCAP], F32, name="tm")
+                nc.vector.tensor_tensor(
+                    out=tm[:],
+                    in0=t_ps[:],
+                    in1=mx[:].unsqueeze(2).to_broadcast([P, a, NCAP]),
+                    op=ALU.subtract,
+                )
+                ex = small.tile([P, a, NCAP], F32, name="ex")
+                nc.scalar.activation(out=ex[:], in_=tm[:], func=ACT.Exp)
+                sm = small.tile([P, a], F32, name="sm")
+                nc.vector.tensor_reduce(out=sm[:], in_=ex[:], axis=AX.X, op=ALU.add)
+                rc = small.tile([P, a], F32, name="rc")
+                nc.vector.reciprocal(out=rc[:], in_=sm[:])
+                c = small.tile([P, a, NCAP], F32, name="c")
+                nc.vector.tensor_tensor(
+                    out=c[:],
+                    in0=ex[:],
+                    in1=rc[:].unsqueeze(2).to_broadcast([P, a, NCAP]),
+                    op=ALU.mult,
+                )
+                v_ps = psum_rt.tile([P, C4, 2], F32, name="v_ps", tag="rt")
+                for bl in range(GB):
+                    for g in range(CG):
+                        for j in range(SJ):
+                            nc.tensor.matmul(
+                                out=v_ps[:, bl * CG + g, :],
+                                lhsT=u[:, bl, 0, j, P * g : P * g + P],
+                                rhs=c[:, bl * SJ + j, 2 * g : 2 * g + 2],
+                                start=(j == 0),
+                                stop=(j == SJ - 1),
+                            )
+                v = small.tile([P, C4], F32, name="v")
+                nc.vector.tensor_copy(out=v[0:64, :], in_=v_ps[0:64, :, 0])
+                nc.vector.tensor_copy(out=v[64:128, :], in_=v_ps[64:128, :, 1])
+
+        for q in range(NGROUPS):
+            u, v0 = project(q)
+            route(q, u, v0)
+
+        of_ps = psum_x.tile([P, P], F32, name="of_ps", tag="xt")
+        nc.tensor.transpose(of_ps[:], ofin[:], ident[:])
+        of_sb = const.tile([P, P], F32, name="of_sb")
+        nc.vector.tensor_copy(out=of_sb[:], in_=of_ps[:])
+        nc.sync.dma_start(
+            out=out.rearrange("b (g n2) d -> (b g) (n2 d)", n2=2), in_=of_sb[0 : B * CG, :]
+        )

@@ -16,11 +16,14 @@ S, B, H, NCAP, DC = 512, 16, 512, 8, 64
 ROUNDS = 4
 P = 128
 SJ = S // P
-CG = NCAP * DC // P
+DH = 4
+DL = DC // DH
 GB = 2
 NGROUPS = B // GB
-C4 = GB * CG
+A = GB * SJ
 EPS = 1e-7
+GPSIMD_DH = (2, 3)
+VECTOR_EVAC_DH = (1, 3)
 
 FLOPS = 2 * S * B * H * NCAP * DC + (2 * ROUNDS - 1) * 2 * S * B * NCAP * DC
 
@@ -31,55 +34,64 @@ def tile_capsule_t_kernel(tc, inputs, W, out):
         const = ctx.enter_context(tc.tile_pool(name="const", bufs=1))
         xpool = ctx.enter_context(tc.tile_pool(name="xpool", bufs=2))
         gpool = ctx.enter_context(tc.tile_pool(name="gpool", bufs=2))
-        qpool = ctx.enter_context(tc.tile_pool(name="qpool", bufs=3))
-        upool = ctx.enter_context(tc.tile_pool(name="upool", bufs=4))
-        small = ctx.enter_context(tc.tile_pool(name="small", bufs=6))
-        psum_x = ctx.enter_context(tc.psum_pool(name="psum_x", bufs=2))
-        psum_mx = ctx.enter_context(tc.psum_pool(name="psum_mx", bufs=3))
-        psum_rt = ctx.enter_context(tc.psum_pool(name="psum_rt", bufs=3))
+        qpool = ctx.enter_context(tc.tile_pool(name="qpool", bufs=2))
+        upool = ctx.enter_context(tc.tile_pool(name="upool", bufs=NGROUPS))
+        wpool = ctx.enter_context(tc.tile_pool(name="wpool", bufs=3))
+        cpool = ctx.enter_context(tc.tile_pool(name="cpool", bufs=3))
+        small = ctx.enter_context(tc.tile_pool(name="small", bufs=NGROUPS + 1))
+        psum = ctx.enter_context(tc.psum_pool(name="psum", bufs=8))
 
         ident = const.tile([P, P], F32, name="ident")
         masks.make_identity(nc, ident[:])
-        blk = const.tile([P, P], F32, name="blk")
-        nc.vector.memset(blk[:], 0.0)
-        nc.vector.memset(blk[0:64, 0:64], 1.0)
-        nc.vector.memset(blk[64:128, 64:128], 1.0)
-        mask = const.tile([P, 2], F32, name="mask")
-        nc.vector.memset(mask[:], 0.0)
-        nc.vector.memset(mask[0:64, 0:1], 1.0)
-        nc.vector.memset(mask[64:128, 1:2], 1.0)
-        neghalf = const.tile([P, C4], F32, name="neghalf")
+        m8 = const.tile([P, NCAP], F32, name="m8")
+        nc.vector.tensor_reduce(
+            out=m8[:], in_=ident[:].rearrange("p (n dl) -> p n dl", dl=DL), axis=AX.X, op=ALU.add
+        )
+        blk = const.tile([P, NCAP, DL], F32, name="blk")
+        nc.vector.tensor_copy(out=blk[:], in_=m8[:].unsqueeze(2).to_broadcast([P, NCAP, DL]))
+        neghalf = const.tile([P, GB], F32, name="neghalf")
         nc.vector.memset(neghalf[:], -0.5)
+        zero = const.tile([P, 1], F32, name="zero")
+        nc.vector.memset(zero[:], 0.0)
         ofin = const.tile([P, P], F32, name="ofin")
         nc.vector.memset(ofin[:], 0.0)
+        junk = const.tile([P, S], F32, name="junk")
 
         wraw = const.tile([P, 4, NCAP * DC], BF16, name="wraw")
         nc.sync.dma_start(
             out=wraw[:].rearrange("p (u e) c -> p u e c", u=2),
             in_=W[0].rearrange("(u p e) c -> p u e c", u=2, e=2),
         )
-        wg = const.tile([P, NCAP * DC, 4], BF16, name="wg", align_bytes=64)
-        nc.vector.tensor_copy(out=wg[:], in_=wraw[:].rearrange("p t c -> p c t"))
+        wg = const.tile([P, DH, NCAP, DL, 4], BF16, name="wg", align_bytes=64)
+        wview = wraw[:].rearrange("p t (n dh dl) -> p dh n dl t", dh=DH, dl=DL)
+        for dh in range(DH):
+            nc.vector.tensor_copy(out=wg[:, dh], in_=wview[:, dh])
         wq = const.tile([P, NCAP * DC], U32, name="wq", align_bytes=64)
         ws = const.tile([P, NCAP * DC], U8, name="ws", align_bytes=64)
         nc.vector.quantize_mx(
-            out=wq[:].bitcast(FP8X4), scales=ws[:], in_=wg[:].rearrange("p c t -> p (c t)")
+            out=wq[:].bitcast(FP8X4),
+            scales=ws[:],
+            in_=wg[:].rearrange("p dh n dl t -> p (dh n dl t)"),
         )
 
         xin = inputs.rearrange("(j p) b h -> p j b h", p=P)
+        us = {}
+        vs = {}
+        ocums = {}
 
         def project(q):
             b0 = q * GB
             x = xpool.tile([P, SJ, GB, H], BF16, name="x")
             nc.sync.dma_start(out=x[:], in_=xin[:, :, b0 : b0 + GB, :])
             x32 = x[:].bitcast(F32)
-            u = upool.tile([P, GB, 2, 4, 512], F32, name="u")
-            v0 = small.tile([P, C4], F32, name="v0")
+            u = upool.tile([P, GB, DH, S], F32, name="u")
+            v0s = small.tile([P, GB, DH], F32, name="v0s")
+            v0 = small.tile([P, GB, DH], F32, name="v")
             for bl in range(GB):
                 grouped = gpool.tile([P, 4 * S], BF16, name="grouped", align_bytes=64)
                 g32 = grouped[:].bitcast(F32)
                 for half in range(2):
-                    xt = psum_x.tile([P, 2, 2, P], F32, name="xt", tag="xt")
+                    xt = psum.tile([P, 2, 2, P], F32, name="xt", tag="ps")
                     for jj in range(2):
                         for uu in range(2):
                             nc.tensor.transpose(
@@ -96,141 +108,181 @@ def tile_capsule_t_kernel(tc, inputs, W, out):
                 xq = qpool.tile([P, S], U32, name="xq", align_bytes=64)
                 xs = qpool.tile([P, S], U8, name="xs", align_bytes=64)
                 nc.vector.quantize_mx(out=xq[:].bitcast(FP8X4), scales=xs[:], in_=grouped[:])
-                for j in range(SJ):
-                    pa = psum_mx.tile([P, 512], F32, name="pa", tag="mx")
-                    nc.tensor.matmul_mx(
-                        out=pa[:],
-                        lhsT=xq[:, P * j : P * j + P].bitcast(FP8X4),
-                        lhsT_scale=xs[:, P * j : P * j + P],
-                        rhs=wq[:].bitcast(FP8X4),
-                        rhs_scale=ws[:],
-                        start=True,
-                        stop=True,
-                    )
-                    nc.vector.tensor_copy(out=u[:, bl, 0, j, :], in_=pa[:])
-                for g in range(CG):
-                    pb = psum_mx.tile([P, 512], F32, name="pb", tag="mx")
+                for dh in range(DH):
+                    pb = psum.tile([P, S], F32, name="pb", tag="ps")
                     nc.tensor.matmul_mx(
                         out=pb[:],
-                        lhsT=wq[:, P * g : P * g + P].bitcast(FP8X4),
-                        lhsT_scale=ws[:, P * g : P * g + P],
+                        lhsT=wq[:, P * dh : P * dh + P].bitcast(FP8X4),
+                        lhsT_scale=ws[:, P * dh : P * dh + P],
                         rhs=xq[:].bitcast(FP8X4),
                         rhs_scale=xs[:],
                         start=True,
                         stop=True,
                     )
-                    col = bl * CG + g
-                    nc.scalar.activation(
-                        out=u[:, bl, 1, g, :],
-                        in_=pb[:],
-                        func=ACT.Copy,
-                        accum_out=v0[:, col : col + 1],
-                    )
-            return u, v0
-
-        def squash(v):
-            sq = small.tile([P, C4], F32, name="sq")
-            nc.vector.tensor_tensor(out=sq[:], in0=v[:], in1=v[:], op=ALU.mult)
-            s_ps = psum_rt.tile([P, C4], F32, name="s_ps", tag="rt")
-            nc.tensor.matmul(out=s_ps[:], lhsT=blk[:], rhs=sq[:], start=True, stop=True)
-            xe = small.tile([P, C4], F32, name="xe")
-            nc.vector.tensor_scalar(
-                out=xe[:], in0=s_ps[:], scalar1=EPS, scalar2=None, op0=ALU.add
-            )
-            rs = small.tile([P, C4], F32, name="rs")
-            nc.gpsimd.tensor_tensor(out=rs[:], in0=xe[:], in1=neghalf[:], op=ALU.pow)
-            return rs
-
-        def route(q, u, v0):
-            oblk = small.tile([P, C4, 2], F32, name="oblk")
-            v = small.tile([P, C4], F32, name="v")
-            nc.vector.tensor_scalar(
-                out=v[:], in0=v0[:], scalar1=1.0 / NCAP, scalar2=None, op0=ALU.mult
-            )
-            for r in range(ROUNDS):
-                rs = squash(v)
-                if r == ROUNDS - 1:
-                    nc.vector.tensor_tensor(
-                        out=ofin[:, q * C4 : (q + 1) * C4], in0=v[:], in1=rs[:], op=ALU.mult
-                    )
-                    break
-                o = small.tile([P, C4], F32, name="o")
-                nc.vector.tensor_tensor(out=o[:], in0=v[:], in1=rs[:], op=ALU.mult)
-                for n2 in range(2):
-                    if r == 0:
+                    if dh in VECTOR_EVAC_DH:
                         nc.vector.tensor_scalar(
-                            out=oblk[:, :, n2],
-                            in0=o[:],
-                            scalar1=mask[:, n2 : n2 + 1],
+                            out=u[:, bl, dh, :],
+                            in0=pb[:],
+                            scalar1=1.0,
                             scalar2=None,
                             op0=ALU.mult,
+                            op1=ALU.add,
+                            accum_out=v0[:, bl, dh : dh + 1],
                         )
                     else:
-                        nc.vector.scalar_tensor_tensor(
-                            out=oblk[:, :, n2],
-                            in0=o[:],
-                            scalar=mask[:, n2 : n2 + 1],
-                            in1=oblk[:, :, n2],
+                        nc.scalar.activation(
+                            out=u[:, bl, dh, :],
+                            in_=pb[:],
+                            func=ACT.Copy,
+                            accum_out=v0s[:, bl, dh : dh + 1],
+                        )
+            nc.vector.tensor_copy(
+                out=v0[:].rearrange("p b (a e) -> p b a e", e=2)[:, :, :, 0],
+                in_=v0s[:].rearrange("p b (a e) -> p b a e", e=2)[:, :, :, 0],
+            )
+            us[q] = u
+            vs[q] = v0
+
+        def routing_round(q, r):
+            u = us[q]
+            v = vs[q]
+            pre = 1.0 / NCAP if r == 0 else 1.0
+            sqj = small.tile([P, GB, DH], F32, name="sqj")
+            ssq = small.tile([P, GB], F32, name="ssq")
+            for bl in range(GB):
+                nc.scalar.activation(
+                    out=sqj[:, bl, :],
+                    in_=v[:, bl, :],
+                    func=ACT.Square,
+                    scale=pre,
+                    accum_out=ssq[:, bl : bl + 1],
+                )
+            n_ps = psum.tile([P, GB], F32, name="n_ps", tag="ps")
+            nc.tensor.matmul(
+                out=n_ps[:],
+                lhsT=blk[:].rearrange("p n dl -> p (n dl)"),
+                rhs=ssq[:],
+                start=True,
+                stop=True,
+            )
+            xe = small.tile([P, GB], F32, name="xe")
+            nc.vector.tensor_scalar(
+                out=xe[:], in0=n_ps[:], scalar1=EPS, scalar2=None, op0=ALU.add
+            )
+            rs = small.tile([P, GB], F32, name="rs")
+            nc.gpsimd.tensor_tensor(out=rs[:], in0=xe[:], in1=neghalf[:], op=ALU.pow)
+            rsb = rs[:].unsqueeze(2).to_broadcast([P, GB, DH])
+            if r == ROUNDS - 1:
+                nc.vector.tensor_tensor(
+                    out=ofin[:, 0 : DH * B].rearrange("p (dh b) -> p b dh", dh=DH)[
+                        :, q * GB : (q + 1) * GB, :
+                    ],
+                    in0=v[:],
+                    in1=rsb,
+                    op=ALU.mult,
+                )
+                return
+            if r == 0:
+                ocum = small.tile([P, GB, DH], F32, name="ocum")
+                nc.vector.scalar_tensor_tensor(
+                    out=ocum[:], in0=v[:], scalar=pre, in1=rsb, op0=ALU.mult, op1=ALU.mult
+                )
+                ocums[q] = ocum
+            else:
+                ocum = ocums[q]
+                o = small.tile([P, GB, DH], F32, name="o")
+                nc.vector.tensor_tensor(out=o[:], in0=v[:], in1=rsb, op=ALU.mult)
+                nc.vector.tensor_tensor(out=ocum[:], in0=ocum[:], in1=o[:], op=ALU.add)
+            t = small.tile([P, A, NCAP], F32, name="t")
+            for bl in range(GB):
+                wt = wpool.tile([P, DH, S], F32, name="wt")
+                for dh in range(DH):
+                    if dh in GPSIMD_DH:
+                        nc.gpsimd.tensor_scalar(
+                            out=wt[:, dh, :],
+                            in0=u[:, bl, dh, :],
+                            scalar1=ocum[:, bl, dh : dh + 1],
+                            scalar2=zero[:, 0:1],
                             op0=ALU.mult,
                             op1=ALU.add,
                         )
-                t_ps = psum_rt.tile([P, GB * SJ, NCAP], F32, name="t_ps", tag="rt")
-                for bl in range(GB):
-                    for j in range(SJ):
-                        for g in range(CG):
-                            nc.tensor.matmul(
-                                out=t_ps[:, bl * SJ + j, 2 * g : 2 * g + 2],
-                                lhsT=u[:, bl, 1, g, P * j : P * j + P],
-                                rhs=oblk[:, bl * CG + g, :],
-                                start=True,
-                                stop=True,
-                            )
-                a = GB * SJ
-                mx = small.tile([P, a], F32, name="mx")
-                nc.vector.tensor_reduce(out=mx[:], in_=t_ps[:], axis=AX.X, op=ALU.max)
-                tm = small.tile([P, a, NCAP], F32, name="tm")
-                nc.vector.tensor_tensor(
-                    out=tm[:],
-                    in0=t_ps[:],
-                    in1=mx[:].unsqueeze(2).to_broadcast([P, a, NCAP]),
-                    op=ALU.subtract,
+                    else:
+                        nc.scalar.activation(
+                            out=wt[:, dh, :],
+                            in_=u[:, bl, dh, :],
+                            func=ACT.Copy,
+                            scale=ocum[:, bl, dh : dh + 1],
+                        )
+                tp = psum.tile([P, SJ, P], F32, name="tp", tag="ps")
+                for j in range(SJ):
+                    for dh in range(DH):
+                        nc.tensor.matmul(
+                            out=tp[:, j, :],
+                            lhsT=wt[:, dh, P * j : P * j + P],
+                            rhs=ident[:],
+                            is_transpose=True,
+                            start=(dh == 0),
+                            stop=(dh == DH - 1),
+                        )
+                nc.vector.tensor_reduce(
+                    out=t[:, bl * SJ : (bl + 1) * SJ, :],
+                    in_=tp[:].rearrange("p j (n dl) -> p j n dl", dl=DL),
+                    axis=AX.X,
+                    op=ALU.add,
                 )
-                ex = small.tile([P, a, NCAP], F32, name="ex")
-                nc.scalar.activation(out=ex[:], in_=tm[:], func=ACT.Exp)
-                sm = small.tile([P, a], F32, name="sm")
-                nc.vector.tensor_reduce(out=sm[:], in_=ex[:], axis=AX.X, op=ALU.add)
-                rc = small.tile([P, a], F32, name="rc")
-                nc.vector.reciprocal(out=rc[:], in_=sm[:])
-                c = small.tile([P, a, NCAP], F32, name="c")
-                nc.vector.tensor_tensor(
-                    out=c[:],
-                    in0=ex[:],
-                    in1=rc[:].unsqueeze(2).to_broadcast([P, a, NCAP]),
-                    op=ALU.mult,
+            nmx = small.tile([P, A], F32, name="nmx")
+            nc.vector.tensor_reduce(out=nmx[:], in_=t[:], axis=AX.X, op=ALU.max, negate=True)
+            ex = small.tile([P, A, NCAP], F32, name="ex")
+            sm = small.tile([P, A], F32, name="sm")
+            for a in range(A):
+                nc.scalar.activation(
+                    out=ex[:, a, :],
+                    in_=t[:, a, :],
+                    func=ACT.Exp,
+                    bias=nmx[:, a : a + 1],
+                    accum_out=sm[:, a : a + 1],
                 )
-                v_ps = psum_rt.tile([P, C4, 2], F32, name="v_ps", tag="rt")
-                for bl in range(GB):
-                    for g in range(CG):
-                        for j in range(SJ):
-                            nc.tensor.matmul(
-                                out=v_ps[:, bl * CG + g, :],
-                                lhsT=u[:, bl, 0, j, P * g : P * g + P],
-                                rhs=c[:, bl * SJ + j, 2 * g : 2 * g + 2],
-                                start=(j == 0),
-                                stop=(j == SJ - 1),
-                            )
-                v = small.tile([P, C4], F32, name="v")
-                nc.vector.tensor_copy(out=v[0:64, :], in_=v_ps[0:64, :, 0])
-                nc.vector.tensor_copy(out=v[64:128, :], in_=v_ps[64:128, :, 1])
+            rc = small.tile([P, A], F32, name="rc")
+            nc.vector.reciprocal(out=rc[:], in_=sm[:])
+            vnew = small.tile([P, GB, DH], F32, name="v")
+            for bl in range(GB):
+                crep = cpool.tile([P, SJ, NCAP, DL], F32, name="crep")
+                for j in range(SJ):
+                    a = bl * SJ + j
+                    nc.scalar.activation(
+                        out=crep[:, j],
+                        in_=ex[:, a, :].unsqueeze(2).to_broadcast([P, NCAP, DL]),
+                        func=ACT.Copy,
+                        scale=rc[:, a : a + 1],
+                    )
+                cb = psum.tile([P, SJ, P], F32, name="cb", tag="ps")
+                for j in range(SJ):
+                    nc.tensor.transpose(
+                        cb[:, j, :], crep[:, j].rearrange("p n dl -> p (n dl)"), ident[:]
+                    )
+                for dh in range(DH):
+                    nc.vector.scalar_tensor_tensor(
+                        out=junk[:],
+                        in0=u[:, bl, dh, :],
+                        scalar=1.0,
+                        in1=cb[:].rearrange("p j s -> p (j s)"),
+                        op0=ALU.mult,
+                        op1=ALU.mult,
+                        accum_out=vnew[:, bl, dh : dh + 1],
+                    )
+            vs[q] = vnew
 
         for q in range(NGROUPS):
-            u, v0 = project(q)
-            route(q, u, v0)
+            project(q)
+        for r in range(ROUNDS):
+            for q in range(NGROUPS):
+                routing_round(q, r)
 
-        of_ps = psum_x.tile([P, P], F32, name="of_ps", tag="xt")
+        of_ps = psum.tile([P, P], F32, name="of_ps", tag="ps")
         nc.tensor.transpose(of_ps[:], ofin[:], ident[:])
-        of_sb = const.tile([P, P], F32, name="of_sb")
-        nc.vector.tensor_copy(out=of_sb[:], in_=of_ps[:])
-        nc.sync.dma_start(
-            out=out.rearrange("b (g n2) d -> (b g) (n2 d)", n2=2), in_=of_sb[0 : B * CG, :]
-        )
+        of_sb = const.tile([P, NCAP, DL], F32, name="of_sb")
+        nc.vector.tensor_copy(out=of_sb[:].rearrange("p n dl -> p (n dl)"), in_=of_ps[:])
+        for dh in range(DH):
+            nc.sync.dma_start(
+                out=out[:, :, DL * dh : DL * dh + DL], in_=of_sb[B * dh : B * dh + B, :, :]
+            )

@@ -19,13 +19,21 @@ SJ = S // P
 DH = 4
 DL = DC // DH
 GB = 2
-NGROUPS = B // GB
+NG = B // GB
 A = GB * SJ
 EPS = 1e-7
-GPSIMD_DH = (2, 3)
-VECTOR_EVAC_DH = (1, 3)
+NU = (ROUNDS - 1) * NG
+FINLAG = 20
+PIN = True
 
 FLOPS = 2 * S * B * H * NCAP * DC + (2 * ROUNDS - 1) * 2 * S * B * NCAP * DC
+
+
+def gpsimd_dh(r):
+    return (0, 1, 2, 3) if r == 0 else (1, 2, 3)
+
+
+VECTOR_EVAC_DH = (1, 3)
 
 
 def tile_capsule_t_kernel(tc, inputs, W, out):
@@ -35,11 +43,15 @@ def tile_capsule_t_kernel(tc, inputs, W, out):
         xpool = ctx.enter_context(tc.tile_pool(name="xpool", bufs=2))
         gpool = ctx.enter_context(tc.tile_pool(name="gpool", bufs=2))
         qpool = ctx.enter_context(tc.tile_pool(name="qpool", bufs=2))
-        upool = ctx.enter_context(tc.tile_pool(name="upool", bufs=NGROUPS))
+        upool = ctx.enter_context(tc.tile_pool(name="upool", bufs=NG))
         wpool = ctx.enter_context(tc.tile_pool(name="wpool", bufs=3))
         cpool = ctx.enter_context(tc.tile_pool(name="cpool", bufs=3))
-        small = ctx.enter_context(tc.tile_pool(name="small", bufs=NGROUPS + 1))
-        psum = ctx.enter_context(tc.psum_pool(name="psum", bufs=8))
+        small = ctx.enter_context(tc.tile_pool(name="small", bufs=NG + 1))
+        psum_pj = ctx.enter_context(tc.psum_pool(name="psum_pj", bufs=4))
+        psum_tp = ctx.enter_context(tc.psum_pool(name="psum_tp", bufs=2))
+        psum_cb = ctx.enter_context(tc.psum_pool(name="psum_cb", bufs=2))
+        if PIN:
+            ctx.enter_context(tc.manual_schedule())
 
         ident = const.tile([P, P], F32, name="ident")
         masks.make_identity(nc, ident[:])
@@ -57,11 +69,30 @@ def tile_capsule_t_kernel(tc, inputs, W, out):
         nc.vector.memset(ofin[:], 0.0)
         junk = const.tile([P, S], F32, name="junk")
 
+        xin = inputs.rearrange("(j p) b h -> p j b h", p=P)
+        st = {}
+        for q in range(NG):
+            st[q] = {}
+
+        def load(q):
+            x = xpool.tile([P, SJ, GB, H], BF16, name="x")
+            nc.sync.dma_start(out=x[:], in_=xin[:, :, q * GB : (q + 1) * GB, :])
+            st[q]["x32"] = x[:].bitcast(F32)
+
+        load(0)
         wraw = const.tile([P, 4, NCAP * DC], BF16, name="wraw")
         nc.sync.dma_start(
             out=wraw[:].rearrange("p (u e) c -> p u e c", u=2),
             in_=W[0].rearrange("(u p e) c -> p u e c", u=2, e=2),
         )
+        load(1)
+        loaded = [2]
+
+        def load_up_to(n):
+            while loaded[0] < min(n, NG):
+                load(loaded[0])
+                loaded[0] += 1
+
         wg = const.tile([P, DH, NCAP, DL, 4], BF16, name="wg", align_bytes=64)
         wview = wraw[:].rearrange("p t (n dh dl) -> p dh n dl t", dh=DH, dl=DL)
         for dh in range(DH):
@@ -74,104 +105,136 @@ def tile_capsule_t_kernel(tc, inputs, W, out):
             in_=wg[:].rearrange("p dh n dl t -> p (dh n dl t)"),
         )
 
-        xin = inputs.rearrange("(j p) b h -> p j b h", p=P)
-        us = {}
-        vs = {}
-        ocums = {}
+        def st_t(q, bl):
+            s = st[q]
+            tiles = []
+            for half in range(2):
+                xt = psum_pj.tile([P, 2, 2, P], F32, name="xt", tag="pj")
+                for jj in range(2):
+                    for uu in range(2):
+                        nc.tensor.transpose(
+                            xt[:, jj, uu, :],
+                            s["x32"][:, 2 * half + jj, bl, P * uu : P * uu + P],
+                            ident[:],
+                        )
+                tiles.append(xt)
+            s["xt", bl] = tiles
 
-        def project(q):
-            b0 = q * GB
-            x = xpool.tile([P, SJ, GB, H], BF16, name="x")
-            nc.sync.dma_start(out=x[:], in_=xin[:, :, b0 : b0 + GB, :])
-            x32 = x[:].bitcast(F32)
-            u = upool.tile([P, GB, DH, S], F32, name="u")
-            v0s = small.tile([P, GB, DH], F32, name="v0s")
-            v0 = small.tile([P, GB, DH], F32, name="v")
-            for bl in range(GB):
-                grouped = gpool.tile([P, 4 * S], BF16, name="grouped", align_bytes=64)
-                g32 = grouped[:].bitcast(F32)
-                for half in range(2):
-                    xt = psum.tile([P, 2, 2, P], F32, name="xt", tag="ps")
-                    for jj in range(2):
-                        for uu in range(2):
-                            nc.tensor.transpose(
-                                xt[:, jj, uu, :],
-                                x32[:, 2 * half + jj, bl, P * uu : P * uu + P],
-                                ident[:],
-                            )
-                    nc.scalar.copy(
-                        out=g32[:, 512 * half : 512 * half + 512].rearrange(
-                            "p (jj s uu) -> p jj s uu", jj=2, uu=2
-                        ),
-                        in_=xt[:].rearrange("p jj uu s -> p jj s uu"),
-                    )
-                xq = qpool.tile([P, S], U32, name="xq", align_bytes=64)
-                xs = qpool.tile([P, S], U8, name="xs", align_bytes=64)
-                nc.vector.quantize_mx(out=xq[:].bitcast(FP8X4), scales=xs[:], in_=grouped[:])
-                for dh in range(DH):
-                    pb = psum.tile([P, S], F32, name="pb", tag="ps")
-                    nc.tensor.matmul_mx(
-                        out=pb[:],
-                        lhsT=wq[:, P * dh : P * dh + P].bitcast(FP8X4),
-                        lhsT_scale=ws[:, P * dh : P * dh + P],
-                        rhs=xq[:].bitcast(FP8X4),
-                        rhs_scale=xs[:],
-                        start=True,
-                        stop=True,
-                    )
-                    if dh in VECTOR_EVAC_DH:
-                        nc.vector.tensor_scalar(
-                            out=u[:, bl, dh, :],
-                            in0=pb[:],
-                            scalar1=1.0,
-                            scalar2=None,
-                            op0=ALU.mult,
-                            op1=ALU.add,
-                            accum_out=v0[:, bl, dh : dh + 1],
-                        )
-                    else:
-                        nc.scalar.activation(
-                            out=u[:, bl, dh, :],
-                            in_=pb[:],
-                            func=ACT.Copy,
-                            accum_out=v0s[:, bl, dh : dh + 1],
-                        )
-            nc.vector.tensor_copy(
-                out=v0[:].rearrange("p b (a e) -> p b a e", e=2)[:, :, :, 0],
-                in_=v0s[:].rearrange("p b (a e) -> p b a e", e=2)[:, :, :, 0],
+        def st_xc(q, bl):
+            s = st[q]
+            grouped = gpool.tile([P, 4 * S], BF16, name="grouped", align_bytes=64)
+            g32 = grouped[:].bitcast(F32)
+            for half in range(2):
+                nc.scalar.copy(
+                    out=g32[:, 512 * half : 512 * half + 512].rearrange(
+                        "p (jj s uu) -> p jj s uu", jj=2, uu=2
+                    ),
+                    in_=s["xt", bl][half][:].rearrange("p jj uu s -> p jj s uu"),
+                )
+            s["grouped", bl] = grouped
+
+        def st_q(q, bl):
+            s = st[q]
+            xq = qpool.tile([P, S], U32, name="xq", align_bytes=64)
+            xs = qpool.tile([P, S], U8, name="xs", align_bytes=64)
+            nc.vector.quantize_mx(
+                out=xq[:].bitcast(FP8X4), scales=xs[:], in_=s["grouped", bl][:]
             )
-            us[q] = u
-            vs[q] = v0
+            s["xq", bl] = (xq, xs)
 
-        def routing_round(q, r):
-            u = us[q]
-            v = vs[q]
+        def st_m(q, bl):
+            s = st[q]
+            xq, xs = s["xq", bl]
+            for dh in range(DH):
+                pb = psum_pj.tile([P, S], F32, name="pb", tag="pj")
+                nc.tensor.matmul_mx(
+                    out=pb[:],
+                    lhsT=wq[:, P * dh : P * dh + P].bitcast(FP8X4),
+                    lhsT_scale=ws[:, P * dh : P * dh + P],
+                    rhs=xq[:].bitcast(FP8X4),
+                    rhs_scale=xs[:],
+                    start=True,
+                    stop=True,
+                )
+                s["pb", bl, dh] = pb
+
+        def st_ev(q, bl):
+            s = st[q]
+            if bl == 0:
+                s["u"] = upool.tile([P, GB, DH, S], F32, name="u")
+                s["v0s"] = small.tile([P, GB, DH], F32, name="v0s")
+                s["v"] = small.tile([P, GB, DH], F32, name="v")
+            for dh in range(DH):
+                if dh in VECTOR_EVAC_DH:
+                    nc.vector.tensor_scalar(
+                        out=s["u"][:, bl, dh, :],
+                        in0=s["pb", bl, dh][:],
+                        scalar1=1.0,
+                        scalar2=None,
+                        op0=ALU.mult,
+                        op1=ALU.add,
+                        accum_out=s["v"][:, bl, dh : dh + 1],
+                    )
+                else:
+                    nc.scalar.activation(
+                        out=s["u"][:, bl, dh, :],
+                        in_=s["pb", bl, dh][:],
+                        func=ACT.Copy,
+                        accum_out=s["v0s"][:, bl, dh : dh + 1],
+                    )
+
+        def st_v0(q):
+            s = st[q]
+            nc.vector.tensor_copy(
+                out=s["v"][:].rearrange("p b (a e) -> p b a e", e=2)[:, :, :, 0],
+                in_=s["v0s"][:].rearrange("p b (a e) -> p b a e", e=2)[:, :, :, 0],
+            )
+
+        def st_a1(q, r):
+            s = st[q]
             pre = 1.0 / NCAP if r == 0 else 1.0
             sqj = small.tile([P, GB, DH], F32, name="sqj")
             ssq = small.tile([P, GB], F32, name="ssq")
             for bl in range(GB):
                 nc.scalar.activation(
                     out=sqj[:, bl, :],
-                    in_=v[:, bl, :],
+                    in_=s["v"][:, bl, :],
                     func=ACT.Square,
                     scale=pre,
                     accum_out=ssq[:, bl : bl + 1],
                 )
-            n_ps = psum.tile([P, GB], F32, name="n_ps", tag="ps")
+            s["ssq"] = ssq
+
+        def st_a2(q):
+            s = st[q]
+            n_ps = psum_pj.tile([P, GB], F32, name="n_ps", tag="pj")
             nc.tensor.matmul(
                 out=n_ps[:],
                 lhsT=blk[:].rearrange("p n dl -> p (n dl)"),
-                rhs=ssq[:],
+                rhs=s["ssq"][:],
                 start=True,
                 stop=True,
             )
+            s["n_ps"] = n_ps
+
+        def st_a3(q):
+            s = st[q]
             xe = small.tile([P, GB], F32, name="xe")
             nc.vector.tensor_scalar(
-                out=xe[:], in0=n_ps[:], scalar1=EPS, scalar2=None, op0=ALU.add
+                out=xe[:], in0=s["n_ps"][:], scalar1=EPS, scalar2=None, op0=ALU.add
             )
+            s["xe"] = xe
+
+        def st_a4(q):
+            s = st[q]
             rs = small.tile([P, GB], F32, name="rs")
-            nc.gpsimd.tensor_tensor(out=rs[:], in0=xe[:], in1=neghalf[:], op=ALU.pow)
-            rsb = rs[:].unsqueeze(2).to_broadcast([P, GB, DH])
+            nc.gpsimd.tensor_tensor(out=rs[:], in0=s["xe"][:], in1=neghalf[:], op=ALU.pow)
+            s["rs"] = rs
+
+        def st_a5(q, r):
+            s = st[q]
+            v = s["v"]
+            rsb = s["rs"][:].unsqueeze(2).to_broadcast([P, GB, DH])
             if r == ROUNDS - 1:
                 nc.vector.tensor_tensor(
                     out=ofin[:, 0 : DH * B].rearrange("p (dh b) -> p b dh", dh=DH)[
@@ -181,104 +244,208 @@ def tile_capsule_t_kernel(tc, inputs, W, out):
                     in1=rsb,
                     op=ALU.mult,
                 )
-                return
-            if r == 0:
+            elif r == 0:
                 ocum = small.tile([P, GB, DH], F32, name="ocum")
                 nc.vector.scalar_tensor_tensor(
-                    out=ocum[:], in0=v[:], scalar=pre, in1=rsb, op0=ALU.mult, op1=ALU.mult
+                    out=ocum[:], in0=v[:], scalar=1.0 / NCAP, in1=rsb, op0=ALU.mult, op1=ALU.mult
                 )
-                ocums[q] = ocum
+                s["ocum"] = ocum
             else:
-                ocum = ocums[q]
                 o = small.tile([P, GB, DH], F32, name="o")
                 nc.vector.tensor_tensor(out=o[:], in0=v[:], in1=rsb, op=ALU.mult)
-                nc.vector.tensor_tensor(out=ocum[:], in0=ocum[:], in1=o[:], op=ALU.add)
-            t = small.tile([P, A, NCAP], F32, name="t")
-            for bl in range(GB):
-                wt = wpool.tile([P, DH, S], F32, name="wt")
+                nc.vector.tensor_tensor(out=s["ocum"][:], in0=s["ocum"][:], in1=o[:], op=ALU.add)
+
+        def st_b(q, r, bl):
+            s = st[q]
+            wt = wpool.tile([P, DH, S], F32, name="wt")
+            for dh in range(DH):
+                if dh in gpsimd_dh(r):
+                    nc.gpsimd.tensor_scalar(
+                        out=wt[:, dh, :],
+                        in0=s["u"][:, bl, dh, :],
+                        scalar1=s["ocum"][:, bl, dh : dh + 1],
+                        scalar2=zero[:, 0:1],
+                        op0=ALU.mult,
+                        op1=ALU.add,
+                    )
+                else:
+                    nc.scalar.activation(
+                        out=wt[:, dh, :],
+                        in_=s["u"][:, bl, dh, :],
+                        func=ACT.Copy,
+                        scale=s["ocum"][:, bl, dh : dh + 1],
+                    )
+            s["wt", bl] = wt
+
+        def st_c(q, bl):
+            s = st[q]
+            tp = psum_tp.tile([P, SJ, P], F32, name="tp", tag="tp")
+            for j in range(SJ):
                 for dh in range(DH):
-                    if dh in GPSIMD_DH:
-                        nc.gpsimd.tensor_scalar(
-                            out=wt[:, dh, :],
-                            in0=u[:, bl, dh, :],
-                            scalar1=ocum[:, bl, dh : dh + 1],
-                            scalar2=zero[:, 0:1],
-                            op0=ALU.mult,
-                            op1=ALU.add,
-                        )
-                    else:
-                        nc.scalar.activation(
-                            out=wt[:, dh, :],
-                            in_=u[:, bl, dh, :],
-                            func=ACT.Copy,
-                            scale=ocum[:, bl, dh : dh + 1],
-                        )
-                tp = psum.tile([P, SJ, P], F32, name="tp", tag="ps")
-                for j in range(SJ):
-                    for dh in range(DH):
-                        nc.tensor.matmul(
-                            out=tp[:, j, :],
-                            lhsT=wt[:, dh, P * j : P * j + P],
-                            rhs=ident[:],
-                            is_transpose=True,
-                            start=(dh == 0),
-                            stop=(dh == DH - 1),
-                        )
-                nc.vector.tensor_reduce(
-                    out=t[:, bl * SJ : (bl + 1) * SJ, :],
-                    in_=tp[:].rearrange("p j (n dl) -> p j n dl", dl=DL),
-                    axis=AX.X,
-                    op=ALU.add,
-                )
+                    nc.tensor.matmul(
+                        out=tp[:, j, :],
+                        lhsT=s["wt", bl][:, dh, P * j : P * j + P],
+                        rhs=ident[:],
+                        is_transpose=True,
+                        start=(dh == 0),
+                        stop=(dh == DH - 1),
+                    )
+            s["tp", bl] = tp
+
+        def st_d(q, bl):
+            s = st[q]
+            if bl == 0:
+                s["t"] = small.tile([P, A, NCAP], F32, name="t")
+            nc.vector.tensor_reduce(
+                out=s["t"][:, bl * SJ : (bl + 1) * SJ, :],
+                in_=s["tp", bl][:].rearrange("p j (n dl) -> p j n dl", dl=DL),
+                axis=AX.X,
+                op=ALU.add,
+            )
+
+        def st_e1(q):
+            s = st[q]
             nmx = small.tile([P, A], F32, name="nmx")
-            nc.vector.tensor_reduce(out=nmx[:], in_=t[:], axis=AX.X, op=ALU.max, negate=True)
+            nc.vector.tensor_reduce(
+                out=nmx[:], in_=s["t"][:], axis=AX.X, op=ALU.max, negate=True
+            )
+            s["nmx"] = nmx
+
+        def st_e2(q):
+            s = st[q]
             ex = small.tile([P, A, NCAP], F32, name="ex")
             sm = small.tile([P, A], F32, name="sm")
             for a in range(A):
                 nc.scalar.activation(
                     out=ex[:, a, :],
-                    in_=t[:, a, :],
+                    in_=s["t"][:, a, :],
                     func=ACT.Exp,
-                    bias=nmx[:, a : a + 1],
+                    bias=s["nmx"][:, a : a + 1],
                     accum_out=sm[:, a : a + 1],
                 )
+            s["ex"] = ex
+            s["sm"] = sm
+
+        def st_e3(q):
+            s = st[q]
             rc = small.tile([P, A], F32, name="rc")
-            nc.vector.reciprocal(out=rc[:], in_=sm[:])
-            vnew = small.tile([P, GB, DH], F32, name="v")
-            for bl in range(GB):
-                crep = cpool.tile([P, SJ, NCAP, DL], F32, name="crep")
-                for j in range(SJ):
-                    a = bl * SJ + j
-                    nc.scalar.activation(
-                        out=crep[:, j],
-                        in_=ex[:, a, :].unsqueeze(2).to_broadcast([P, NCAP, DL]),
-                        func=ACT.Copy,
-                        scale=rc[:, a : a + 1],
-                    )
-                cb = psum.tile([P, SJ, P], F32, name="cb", tag="ps")
-                for j in range(SJ):
-                    nc.tensor.transpose(
-                        cb[:, j, :], crep[:, j].rearrange("p n dl -> p (n dl)"), ident[:]
-                    )
-                for dh in range(DH):
-                    nc.vector.scalar_tensor_tensor(
-                        out=junk[:],
-                        in0=u[:, bl, dh, :],
-                        scalar=1.0,
-                        in1=cb[:].rearrange("p j s -> p (j s)"),
-                        op0=ALU.mult,
-                        op1=ALU.mult,
-                        accum_out=vnew[:, bl, dh : dh + 1],
-                    )
-            vs[q] = vnew
+            nc.vector.reciprocal(out=rc[:], in_=s["sm"][:])
+            s["rc"] = rc
 
-        for q in range(NGROUPS):
-            project(q)
-        for r in range(ROUNDS):
-            for q in range(NGROUPS):
-                routing_round(q, r)
+        def st_e4(q, bl):
+            s = st[q]
+            crep = cpool.tile([P, SJ, NCAP, DL], F32, name="crep")
+            for j in range(SJ):
+                a = bl * SJ + j
+                nc.scalar.activation(
+                    out=crep[:, j],
+                    in_=s["ex"][:, a, :].unsqueeze(2).to_broadcast([P, NCAP, DL]),
+                    func=ACT.Copy,
+                    scale=s["rc"][:, a : a + 1],
+                )
+            s["crep", bl] = crep
 
-        of_ps = psum.tile([P, P], F32, name="of_ps", tag="ps")
+        def st_f(q, bl):
+            s = st[q]
+            cb = psum_cb.tile([P, SJ, P], F32, name="cb", tag="cb")
+            for j in range(SJ):
+                nc.tensor.transpose(
+                    cb[:, j, :], s["crep", bl][:, j].rearrange("p n dl -> p (n dl)"), ident[:]
+                )
+            s["cb", bl] = cb
+
+        def st_g(q, bl):
+            s = st[q]
+            if bl == 0:
+                s["vnew"] = small.tile([P, GB, DH], F32, name="v")
+            for dh in range(DH):
+                nc.vector.scalar_tensor_tensor(
+                    out=junk[:],
+                    in0=s["u"][:, bl, dh, :],
+                    scalar=1.0,
+                    in1=s["cb", bl][:].rearrange("p j s -> p (j s)"),
+                    op0=ALU.mult,
+                    op1=ALU.mult,
+                    accum_out=s["vnew"][:, bl, dh : dh + 1],
+                )
+            if bl == GB - 1:
+                s["v"] = s["vnew"]
+
+        def unit(k):
+            return (k // NG, k % NG)
+
+        def is_unit(k):
+            return 0 <= k < NU
+
+        def squashes(t):
+            found = []
+            if is_unit(t):
+                found.append(unit(t))
+            if 0 <= t - FINLAG < NG:
+                found.append((ROUNDS - 1, t - FINLAG))
+            return found
+
+        for t in range(-3, FINLAG + NG + 1):
+            g2 = t + 2
+            g3 = t + 3
+            pm = 0 <= g2 < NG
+            pt = 0 <= g3 < NG
+            if pt:
+                load_up_to(g3 + 2)
+            if pm:
+                st_m(g2, 0)
+            if is_unit(t - 2):
+                q = unit(t - 2)[1]
+                st_d(q, 0)
+                st_d(q, 1)
+                st_e1(q)
+            for r, q in squashes(t):
+                st_a3(q)
+                st_a4(q)
+            if is_unit(t - 2):
+                st_e2(unit(t - 2)[1])
+            if pm:
+                st_ev(g2, 0)
+            if pt:
+                st_t(g3, 0)
+                st_xc(g3, 0)
+                st_t(g3, 1)
+                st_xc(g3, 1)
+            if is_unit(t - 1):
+                q = unit(t - 1)[1]
+                st_c(q, 0)
+                st_c(q, 1)
+            if is_unit(t - 3):
+                st_g(unit(t - 3)[1], 0)
+            if is_unit(t - 2):
+                st_e3(unit(t - 2)[1])
+            for r, q in squashes(t):
+                st_a5(q, r)
+            if pm:
+                st_m(g2, 1)
+                st_ev(g2, 1)
+                st_v0(g2)
+            if is_unit(t - 2):
+                q = unit(t - 2)[1]
+                st_e4(q, 0)
+                st_e4(q, 1)
+                st_f(q, 0)
+            if is_unit(t - 3):
+                st_g(unit(t - 3)[1], 1)
+            for r, q in squashes(t + 1):
+                st_a1(q, r)
+                st_a2(q)
+            if is_unit(t - 2):
+                st_f(unit(t - 2)[1], 1)
+            for r, q in squashes(t):
+                if r < ROUNDS - 1:
+                    st_b(q, r, 0)
+                    st_b(q, r, 1)
+            if pt:
+                st_q(g3, 0)
+                st_q(g3, 1)
+
+        of_ps = psum_pj.tile([P, P], F32, name="of_ps", tag="pj")
         nc.tensor.transpose(of_ps[:], ofin[:], ident[:])
         of_sb = const.tile([P, NCAP, DL], F32, name="of_sb")
         nc.vector.tensor_copy(out=of_sb[:].rearrange("p n dl -> p (n dl)"), in_=of_ps[:])

@@ -24,13 +24,10 @@ A = GB * SJ
 EPS = 1e-7
 NU = (ROUNDS - 1) * NG
 FINLAG = 20
+LEAD = 8
 PIN = True
 
 FLOPS = 2 * S * B * H * NCAP * DC + (2 * ROUNDS - 1) * 2 * S * B * NCAP * DC
-
-
-def gpsimd_dh(r):
-    return (0, 1, 2, 3) if r == 0 else (1, 2, 3)
 
 
 VECTOR_EVAC_DH = (1, 3)
@@ -44,12 +41,12 @@ def tile_capsule_t_kernel(tc, inputs, W, out):
         gpool = ctx.enter_context(tc.tile_pool(name="gpool", bufs=2))
         qpool = ctx.enter_context(tc.tile_pool(name="qpool", bufs=2))
         upool = ctx.enter_context(tc.tile_pool(name="upool", bufs=NG))
-        wpool = ctx.enter_context(tc.tile_pool(name="wpool", bufs=3))
+        wpool = ctx.enter_context(tc.tile_pool(name="wpool", bufs=4))
         cpool = ctx.enter_context(tc.tile_pool(name="cpool", bufs=3))
         small = ctx.enter_context(tc.tile_pool(name="small", bufs=NG + 1))
-        psum_pj = ctx.enter_context(tc.psum_pool(name="psum_pj", bufs=4))
-        psum_tp = ctx.enter_context(tc.psum_pool(name="psum_tp", bufs=2))
-        psum_cb = ctx.enter_context(tc.psum_pool(name="psum_cb", bufs=2))
+        psum_n = ctx.enter_context(tc.psum_pool(name="psum_n", bufs=1))
+        psum_x = ctx.enter_context(tc.psum_pool(name="psum_x", bufs=4))
+        psum_y = ctx.enter_context(tc.psum_pool(name="psum_y", bufs=3))
         if PIN:
             ctx.enter_context(tc.manual_schedule())
 
@@ -65,6 +62,8 @@ def tile_capsule_t_kernel(tc, inputs, W, out):
         nc.vector.memset(neghalf[:], -0.5)
         zero = const.tile([P, 1], F32, name="zero")
         nc.vector.memset(zero[:], 0.0)
+        epsc = const.tile([P, 1], F32, name="epsc")
+        nc.vector.memset(epsc[:], EPS)
         ofin = const.tile([P, P], F32, name="ofin")
         nc.vector.memset(ofin[:], 0.0)
         junk = const.tile([P, S], F32, name="junk")
@@ -109,7 +108,7 @@ def tile_capsule_t_kernel(tc, inputs, W, out):
             s = st[q]
             tiles = []
             for half in range(2):
-                xt = psum_pj.tile([P, 2, 2, P], F32, name="xt", tag="pj")
+                xt = psum_y.tile([P, 2, 2, P], F32, name="xt", tag="Y")
                 for jj in range(2):
                     for uu in range(2):
                         nc.tensor.transpose(
@@ -142,11 +141,15 @@ def tile_capsule_t_kernel(tc, inputs, W, out):
             )
             s["xq", bl] = (xq, xs)
 
-        def st_m(q, bl):
+        def st_mev(q, bl):
             s = st[q]
             xq, xs = s["xq", bl]
+            if bl == 0:
+                s["u"] = upool.tile([P, GB, DH, S], F32, name="u")
+                s["v0s"] = small.tile([P, GB, DH], F32, name="v0s")
+                s["v"] = small.tile([P, GB, DH], F32, name="v")
             for dh in range(DH):
-                pb = psum_pj.tile([P, S], F32, name="pb", tag="pj")
+                pb = psum_x.tile([P, S], F32, name="pb", tag="X")
                 nc.tensor.matmul_mx(
                     out=pb[:],
                     lhsT=wq[:, P * dh : P * dh + P].bitcast(FP8X4),
@@ -157,14 +160,6 @@ def tile_capsule_t_kernel(tc, inputs, W, out):
                     stop=True,
                 )
                 s["pb", bl, dh] = pb
-
-        def st_ev(q, bl):
-            s = st[q]
-            if bl == 0:
-                s["u"] = upool.tile([P, GB, DH, S], F32, name="u")
-                s["v0s"] = small.tile([P, GB, DH], F32, name="v0s")
-                s["v"] = small.tile([P, GB, DH], F32, name="v")
-            for dh in range(DH):
                 if dh in VECTOR_EVAC_DH:
                     nc.vector.tensor_scalar(
                         out=s["u"][:, bl, dh, :],
@@ -207,7 +202,7 @@ def tile_capsule_t_kernel(tc, inputs, W, out):
 
         def st_a2(q):
             s = st[q]
-            n_ps = psum_pj.tile([P, GB], F32, name="n_ps", tag="pj")
+            n_ps = psum_n.tile([P, GB], F32, name="n_ps", tag="n")
             nc.tensor.matmul(
                 out=n_ps[:],
                 lhsT=blk[:].rearrange("p n dl -> p (n dl)"),
@@ -220,8 +215,8 @@ def tile_capsule_t_kernel(tc, inputs, W, out):
         def st_a3(q):
             s = st[q]
             xe = small.tile([P, GB], F32, name="xe")
-            nc.vector.tensor_scalar(
-                out=xe[:], in0=s["n_ps"][:], scalar1=EPS, scalar2=None, op0=ALU.add
+            nc.scalar.activation(
+                out=xe[:], in_=s["n_ps"][:], func=ACT.Identity, bias=epsc[:, 0:1]
             )
             s["xe"] = xe
 
@@ -236,7 +231,7 @@ def tile_capsule_t_kernel(tc, inputs, W, out):
             v = s["v"]
             rsb = s["rs"][:].unsqueeze(2).to_broadcast([P, GB, DH])
             if r == ROUNDS - 1:
-                nc.vector.tensor_tensor(
+                nc.gpsimd.tensor_tensor(
                     out=ofin[:, 0 : DH * B].rearrange("p (dh b) -> p b dh", dh=DH)[
                         :, q * GB : (q + 1) * GB, :
                     ],
@@ -244,51 +239,51 @@ def tile_capsule_t_kernel(tc, inputs, W, out):
                     in1=rsb,
                     op=ALU.mult,
                 )
-            elif r == 0:
+                return
+            o = small.tile([P, GB, DH], F32, name="o")
+            nc.gpsimd.tensor_tensor(out=o[:], in0=v[:], in1=rsb, op=ALU.mult)
+            if r == 0:
                 ocum = small.tile([P, GB, DH], F32, name="ocum")
-                nc.vector.scalar_tensor_tensor(
-                    out=ocum[:], in0=v[:], scalar=1.0 / NCAP, in1=rsb, op0=ALU.mult, op1=ALU.mult
+                nc.gpsimd.tensor_scalar(
+                    out=ocum[:], in0=o[:], scalar1=1.0 / NCAP, scalar2=0.0, op0=ALU.mult, op1=ALU.add
                 )
                 s["ocum"] = ocum
             else:
-                o = small.tile([P, GB, DH], F32, name="o")
-                nc.vector.tensor_tensor(out=o[:], in0=v[:], in1=rsb, op=ALU.mult)
-                nc.vector.tensor_tensor(out=s["ocum"][:], in0=s["ocum"][:], in1=o[:], op=ALU.add)
+                nc.gpsimd.tensor_tensor(out=s["ocum"][:], in0=s["ocum"][:], in1=o[:], op=ALU.add)
 
         def st_b(q, r, bl):
             s = st[q]
             wt = wpool.tile([P, DH, S], F32, name="wt")
-            for dh in range(DH):
-                if dh in gpsimd_dh(r):
-                    nc.gpsimd.tensor_scalar(
-                        out=wt[:, dh, :],
-                        in0=s["u"][:, bl, dh, :],
-                        scalar1=s["ocum"][:, bl, dh : dh + 1],
-                        scalar2=zero[:, 0:1],
-                        op0=ALU.mult,
-                        op1=ALU.add,
-                    )
-                else:
-                    nc.scalar.activation(
-                        out=wt[:, dh, :],
-                        in_=s["u"][:, bl, dh, :],
-                        func=ACT.Copy,
-                        scale=s["ocum"][:, bl, dh : dh + 1],
-                    )
+            nc.gpsimd.tensor_scalar(
+                out=wt[:, 2, :],
+                in0=s["u"][:, bl, 3, :],
+                scalar1=s["ocum"][:, bl, 3:4],
+                scalar2=zero[:, 0:1],
+                op0=ALU.mult,
+                op1=ALU.add,
+            )
+            for dh, slot in ((2, 3), (0, 0), (1, 1)):
+                nc.scalar.activation(
+                    out=wt[:, slot, :],
+                    in_=s["u"][:, bl, dh, :],
+                    func=ACT.Copy,
+                    scale=s["ocum"][:, bl, dh : dh + 1],
+                )
+            nc.gpsimd.tensor_tensor(out=wt[:, 2, :], in0=wt[:, 2, :], in1=wt[:, 3, :], op=ALU.add)
             s["wt", bl] = wt
 
         def st_c(q, bl):
             s = st[q]
-            tp = psum_tp.tile([P, SJ, P], F32, name="tp", tag="tp")
+            tp = psum_y.tile([P, SJ, P], F32, name="tp", tag="Y")
             for j in range(SJ):
-                for dh in range(DH):
+                for slot in range(3):
                     nc.tensor.matmul(
                         out=tp[:, j, :],
-                        lhsT=s["wt", bl][:, dh, P * j : P * j + P],
+                        lhsT=s["wt", bl][:, slot, P * j : P * j + P],
                         rhs=ident[:],
                         is_transpose=True,
-                        start=(dh == 0),
-                        stop=(dh == DH - 1),
+                        start=(slot == 0),
+                        stop=(slot == 2),
                     )
             s["tp", bl] = tp
 
@@ -347,7 +342,7 @@ def tile_capsule_t_kernel(tc, inputs, W, out):
 
         def st_f(q, bl):
             s = st[q]
-            cb = psum_cb.tile([P, SJ, P], F32, name="cb", tag="cb")
+            cb = psum_x.tile([P, SJ, P], F32, name="cb", tag="X")
             for j in range(SJ):
                 nc.tensor.transpose(
                     cb[:, j, :], s["crep", bl][:, j].rearrange("p n dl -> p (n dl)"), ident[:]
@@ -377,40 +372,53 @@ def tile_capsule_t_kernel(tc, inputs, W, out):
         def is_unit(k):
             return 0 <= k < NU
 
-        def squashes(t):
+        def squashes(k):
             found = []
-            if is_unit(t):
-                found.append(unit(t))
-            if 0 <= t - FINLAG < NG:
-                found.append((ROUNDS - 1, t - FINLAG))
+            if is_unit(k):
+                found.append(unit(k))
+            if 0 <= k - 1 - FINLAG < NG:
+                found.append((ROUNDS - 1, k - 1 - FINLAG))
             return found
 
-        for t in range(-3, FINLAG + NG + 1):
-            g2 = t + 2
-            g3 = t + 3
-            pm = 0 <= g2 < NG
-            pt = 0 <= g3 < NG
-            if pt:
-                load_up_to(g3 + 2)
-            if pm:
-                st_m(g2, 0)
+        def is_batch(b):
+            return 0 <= b < B
+
+        step = [-2]
+
+        def proj_step():
+            b = step[0]
+            step[0] += 1
+            if is_batch(b + 2) and (b + 2) % GB == 0:
+                load_up_to((b + 2) // GB + 2)
+            if is_batch(b + 1):
+                st_q((b + 1) // GB, (b + 1) % GB)
+            if is_batch(b):
+                st_mev(b // GB, b % GB)
+                if b % GB == GB - 1:
+                    st_v0(b // GB)
+            if is_batch(b + 2):
+                st_t((b + 2) // GB, (b + 2) % GB)
+                st_xc((b + 2) // GB, (b + 2) % GB)
+
+        while step[0] < LEAD:
+            proj_step()
+
+        for t in range(-2, FINLAG + NG + 2):
+            if is_unit(t):
+                r, q = unit(t)
+                st_b(q, r, 0)
+                st_b(q, r, 1)
             if is_unit(t - 2):
                 q = unit(t - 2)[1]
                 st_d(q, 0)
                 st_d(q, 1)
                 st_e1(q)
-            for r, q in squashes(t):
+            for r, q in squashes(t + 1):
                 st_a3(q)
                 st_a4(q)
             if is_unit(t - 2):
                 st_e2(unit(t - 2)[1])
-            if pm:
-                st_ev(g2, 0)
-            if pt:
-                st_t(g3, 0)
-                st_xc(g3, 0)
-                st_t(g3, 1)
-                st_xc(g3, 1)
+            proj_step()
             if is_unit(t - 1):
                 q = unit(t - 1)[1]
                 st_c(q, 0)
@@ -418,34 +426,23 @@ def tile_capsule_t_kernel(tc, inputs, W, out):
             if is_unit(t - 3):
                 st_g(unit(t - 3)[1], 0)
             if is_unit(t - 2):
-                st_e3(unit(t - 2)[1])
-            for r, q in squashes(t):
-                st_a5(q, r)
-            if pm:
-                st_m(g2, 1)
-                st_ev(g2, 1)
-                st_v0(g2)
-            if is_unit(t - 2):
                 q = unit(t - 2)[1]
+                st_e3(q)
                 st_e4(q, 0)
                 st_e4(q, 1)
                 st_f(q, 0)
+            proj_step()
             if is_unit(t - 3):
                 st_g(unit(t - 3)[1], 1)
             for r, q in squashes(t + 1):
+                st_a5(q, r)
+            for r, q in squashes(t + 2):
                 st_a1(q, r)
                 st_a2(q)
             if is_unit(t - 2):
                 st_f(unit(t - 2)[1], 1)
-            for r, q in squashes(t):
-                if r < ROUNDS - 1:
-                    st_b(q, r, 0)
-                    st_b(q, r, 1)
-            if pt:
-                st_q(g3, 0)
-                st_q(g3, 1)
 
-        of_ps = psum_pj.tile([P, P], F32, name="of_ps", tag="pj")
+        of_ps = psum_y.tile([P, P], F32, name="of_ps", tag="Y")
         nc.tensor.transpose(of_ps[:], ofin[:], ident[:])
         of_sb = const.tile([P, NCAP, DL], F32, name="of_sb")
         nc.vector.tensor_copy(out=of_sb[:].rearrange("p n dl -> p (n dl)"), in_=of_ps[:])

@@ -23,11 +23,15 @@ NG = B // GB
 A = GB * SJ
 EPS = 1e-7
 NU = (ROUNDS - 1) * NG
-FINLAG = 20
+FINLAG = 22
 LEAD = 8
 PIN = True
 
 FLOPS = 2 * S * B * H * NCAP * DC + (2 * ROUNDS - 1) * 2 * S * B * NCAP * DC
+
+
+def gpsimd_dh(r):
+    return (2, 3)
 
 
 VECTOR_EVAC_DH = (1, 3)
@@ -254,36 +258,37 @@ def tile_capsule_t_kernel(tc, inputs, W, out):
         def st_b(q, r, bl):
             s = st[q]
             wt = wpool.tile([P, DH, S], F32, name="wt")
-            nc.gpsimd.tensor_scalar(
-                out=wt[:, 2, :],
-                in0=s["u"][:, bl, 3, :],
-                scalar1=s["ocum"][:, bl, 3:4],
-                scalar2=zero[:, 0:1],
-                op0=ALU.mult,
-                op1=ALU.add,
-            )
-            for dh, slot in ((2, 3), (0, 0), (1, 1)):
-                nc.scalar.activation(
-                    out=wt[:, slot, :],
-                    in_=s["u"][:, bl, dh, :],
-                    func=ACT.Copy,
-                    scale=s["ocum"][:, bl, dh : dh + 1],
-                )
-            nc.gpsimd.tensor_tensor(out=wt[:, 2, :], in0=wt[:, 2, :], in1=wt[:, 3, :], op=ALU.add)
+            for dh in range(DH):
+                if dh in gpsimd_dh(r):
+                    nc.gpsimd.tensor_scalar(
+                        out=wt[:, dh, :],
+                        in0=s["u"][:, bl, dh, :],
+                        scalar1=s["ocum"][:, bl, dh : dh + 1],
+                        scalar2=zero[:, 0:1],
+                        op0=ALU.mult,
+                        op1=ALU.add,
+                    )
+                else:
+                    nc.scalar.activation(
+                        out=wt[:, dh, :],
+                        in_=s["u"][:, bl, dh, :],
+                        func=ACT.Copy,
+                        scale=s["ocum"][:, bl, dh : dh + 1],
+                    )
             s["wt", bl] = wt
 
         def st_c(q, bl):
             s = st[q]
             tp = psum_y.tile([P, SJ, P], F32, name="tp", tag="Y")
             for j in range(SJ):
-                for slot in range(3):
+                for dh in range(DH):
                     nc.tensor.matmul(
                         out=tp[:, j, :],
-                        lhsT=s["wt", bl][:, slot, P * j : P * j + P],
+                        lhsT=s["wt", bl][:, dh, P * j : P * j + P],
                         rhs=ident[:],
                         is_transpose=True,
-                        start=(slot == 0),
-                        stop=(slot == 2),
+                        start=(dh == 0),
+                        stop=(dh == DH - 1),
                     )
             s["tp", bl] = tp
 
@@ -404,6 +409,8 @@ def tile_capsule_t_kernel(tc, inputs, W, out):
             proj_step()
 
         for t in range(-2, FINLAG + NG + 2):
+            for r, q in squashes(t + 2):
+                st_a1(q, r)
             if is_unit(t):
                 r, q = unit(t)
                 st_b(q, r, 0)
@@ -412,35 +419,36 @@ def tile_capsule_t_kernel(tc, inputs, W, out):
                 q = unit(t - 2)[1]
                 st_d(q, 0)
                 st_d(q, 1)
-                st_e1(q)
             for r, q in squashes(t + 1):
                 st_a3(q)
                 st_a4(q)
-            if is_unit(t - 2):
-                st_e2(unit(t - 2)[1])
             proj_step()
             if is_unit(t - 1):
                 q = unit(t - 1)[1]
                 st_c(q, 0)
                 st_c(q, 1)
             if is_unit(t - 3):
-                st_g(unit(t - 3)[1], 0)
+                q = unit(t - 3)[1]
+                st_f(q, 0)
+                st_f(q, 1)
+            if is_unit(t - 4):
+                st_g(unit(t - 4)[1], 0)
+            if is_unit(t - 2):
+                q = unit(t - 2)[1]
+                st_e1(q)
+                st_e2(q)
+            proj_step()
+            if is_unit(t - 4):
+                st_g(unit(t - 4)[1], 1)
             if is_unit(t - 2):
                 q = unit(t - 2)[1]
                 st_e3(q)
                 st_e4(q, 0)
                 st_e4(q, 1)
-                st_f(q, 0)
-            proj_step()
-            if is_unit(t - 3):
-                st_g(unit(t - 3)[1], 1)
             for r, q in squashes(t + 1):
                 st_a5(q, r)
             for r, q in squashes(t + 2):
-                st_a1(q, r)
                 st_a2(q)
-            if is_unit(t - 2):
-                st_f(unit(t - 2)[1], 1)
 
         of_ps = psum_y.tile([P, P], F32, name="of_ps", tag="Y")
         nc.tensor.transpose(of_ps[:], ofin[:], ident[:])

@@ -23,7 +23,7 @@ NG = B // GB
 A = GB * SJ
 EPS = 1e-7
 NU = (ROUNDS - 1) * NG
-FINLAG = 22
+FINLAG = 23
 LEAD = 8
 PIN = True
 
@@ -47,6 +47,7 @@ def tile_capsule_t_kernel(tc, inputs, W, out):
         upool = ctx.enter_context(tc.tile_pool(name="upool", bufs=NG))
         wpool = ctx.enter_context(tc.tile_pool(name="wpool", bufs=4))
         cpool = ctx.enter_context(tc.tile_pool(name="cpool", bufs=3))
+        opool = ctx.enter_context(tc.tile_pool(name="opool", bufs=2))
         small = ctx.enter_context(tc.tile_pool(name="small", bufs=NG + 1))
         psum_n = ctx.enter_context(tc.psum_pool(name="psum_n", bufs=1))
         psum_x = ctx.enter_context(tc.psum_pool(name="psum_x", bufs=4))
@@ -71,6 +72,7 @@ def tile_capsule_t_kernel(tc, inputs, W, out):
         ofin = const.tile([P, P], F32, name="ofin")
         nc.vector.memset(ofin[:], 0.0)
         junk = const.tile([P, S], F32, name="junk")
+        junk_s = const.tile([P, S], F32, name="junk_s")
 
         xin = inputs.rearrange("(j p) b h -> p j b h", p=P)
         st = {}
@@ -357,8 +359,8 @@ def tile_capsule_t_kernel(tc, inputs, W, out):
         def st_g(q, bl):
             s = st[q]
             if bl == 0:
-                s["vnew"] = small.tile([P, GB, DH], F32, name="v")
-            for dh in range(DH):
+                s["vv"] = small.tile([P, GB, DH], F32, name="vv")
+            for dh in range(DH - bl):
                 nc.vector.scalar_tensor_tensor(
                     out=junk[:],
                     in0=s["u"][:, bl, dh, :],
@@ -366,10 +368,26 @@ def tile_capsule_t_kernel(tc, inputs, W, out):
                     in1=s["cb", bl][:].rearrange("p j s -> p (j s)"),
                     op0=ALU.mult,
                     op1=ALU.mult,
-                    accum_out=s["vnew"][:, bl, dh : dh + 1],
+                    accum_out=s["vv"][:, bl, dh : dh + 1],
                 )
-            if bl == GB - 1:
-                s["v"] = s["vnew"]
+
+        def st_go12(q):
+            s = st[q]
+            cbs = opool.tile([P, S], F32, name="cbs")
+            nc.scalar.copy(out=cbs[:], in_=s["cb", 1][:].rearrange("p j s -> p (j s)"))
+            prod = opool.tile([P, S], F32, name="prod")
+            nc.gpsimd.tensor_tensor(out=prod[:], in0=s["u"][:, 1, 3, :], in1=cbs[:], op=ALU.mult)
+            s["prod"] = prod
+
+        def st_go3(q):
+            s = st[q]
+            v = small.tile([P, GB, DH], F32, name="v")
+            nc.scalar.activation(
+                out=junk_s[:], in_=s["prod"][:], func=ACT.Copy, accum_out=v[:, 1, 3:4]
+            )
+            nc.scalar.copy(out=v[:, 0, :], in_=s["vv"][:, 0, :])
+            nc.scalar.copy(out=v[:, 1, 0:3], in_=s["vv"][:, 1, 0:3])
+            s["v"] = v
 
         def unit(k):
             return (k // NG, k % NG)
@@ -415,6 +433,8 @@ def tile_capsule_t_kernel(tc, inputs, W, out):
                 r, q = unit(t)
                 st_b(q, r, 0)
                 st_b(q, r, 1)
+            if is_unit(t - 4):
+                st_go12(unit(t - 4)[1])
             if is_unit(t - 2):
                 q = unit(t - 2)[1]
                 st_d(q, 0)
@@ -445,6 +465,8 @@ def tile_capsule_t_kernel(tc, inputs, W, out):
                 st_e3(q)
                 st_e4(q, 0)
                 st_e4(q, 1)
+            if is_unit(t - 4):
+                st_go3(unit(t - 4)[1])
             for r, q in squashes(t + 1):
                 st_a5(q, r)
             for r, q in squashes(t + 2):

@@ -191,6 +191,18 @@ def tile_capsule_t_kernel(tc, inputs, W, out):
                 in_=s["v0s"][:].rearrange("p b (a e) -> p b a e", e=2)[:, :, :, 0],
             )
 
+        def keep_clock(bank, passes):
+            for i in range(passes):
+                nc.tensor.matmul_mx(
+                    out=bank[:].rearrange("p j c -> p (j c)"),
+                    lhsT=wq[:, 0:P].bitcast(FP8X4),
+                    lhsT_scale=ws[:, 0:P],
+                    rhs=wq[:].bitcast(FP8X4),
+                    rhs_scale=ws[:],
+                    start=True,
+                    stop=True,
+                )
+
         def st_a1(q, r):
             s = st[q]
             pre = 1.0 / NCAP if r == 0 else 1.0
@@ -279,9 +291,10 @@ def tile_capsule_t_kernel(tc, inputs, W, out):
                     )
             s["wt", bl] = wt
 
-        def st_c(q, bl):
+        def st_c(q, bl, passes):
             s = st[q]
             tp = psum_y.tile([P, SJ, P], F32, name="tp", tag="Y")
+            keep_clock(tp, passes)
             for j in range(SJ):
                 for dh in range(DH):
                     nc.tensor.matmul(
@@ -347,14 +360,19 @@ def tile_capsule_t_kernel(tc, inputs, W, out):
                 )
             s["crep", bl] = crep
 
-        def st_f(q, bl):
+        def st_f(q):
             s = st[q]
-            cb = psum_x.tile([P, SJ, P], F32, name="cb", tag="X")
-            for j in range(SJ):
-                nc.tensor.transpose(
-                    cb[:, j, :], s["crep", bl][:, j].rearrange("p n dl -> p (n dl)"), ident[:]
-                )
-            s["cb", bl] = cb
+            for bl in range(GB):
+                s["cb", bl] = psum_x.tile([P, SJ, P], F32, name="cb", tag="X")
+            keep_clock(s["cb", 0], 2)
+            keep_clock(s["cb", 1], 1)
+            for bl in range(GB):
+                for j in range(SJ):
+                    nc.tensor.transpose(
+                        s["cb", bl][:, j, :],
+                        s["crep", bl][:, j].rearrange("p n dl -> p (n dl)"),
+                        ident[:],
+                    )
 
         def st_g(q, bl):
             s = st[q]
@@ -445,12 +463,11 @@ def tile_capsule_t_kernel(tc, inputs, W, out):
             proj_step()
             if is_unit(t - 1):
                 q = unit(t - 1)[1]
-                st_c(q, 0)
-                st_c(q, 1)
+                passes = 2 if step[0] >= B else 0
+                st_c(q, 0, passes)
+                st_c(q, 1, passes)
             if is_unit(t - 3):
-                q = unit(t - 3)[1]
-                st_f(q, 0)
-                st_f(q, 1)
+                st_f(unit(t - 3)[1])
             if is_unit(t - 4):
                 st_g(unit(t - 4)[1], 0)
             if is_unit(t - 2):

from contextlib import ExitStack

import concourse.masks as masks
import concourse.mybir as mybir

F32 = mybir.dt.float32
BF16 = mybir.dt.bfloat16
U32 = mybir.dt.uint32
U8 = mybir.dt.uint8
FP8X4 = mybir.dt.float8_e4m3fn_x4
ALU = mybir.AluOpType
ACT = mybir.ActivationFunctionType
AX = mybir.AxisListType

S, B, H, NCAP, DC = 512, 16, 512, 8, 64
ROUNDS = 4
P = 128
SJ = S // P
DH = 4
DL = DC // DH
GB = 2
NG = B // GB
A = GB * SJ
EPS = 1e-7
NU = (ROUNDS - 1) * NG
FINLAG = 23
LEAD = 8
PIN = True

FLOPS = 2 * S * B * H * NCAP * DC + (2 * ROUNDS - 1) * 2 * S * B * NCAP * DC


def gpsimd_dh(r):
    return (2, 3)


VECTOR_EVAC_DH = (1, 3)


def tile_capsule_t_kernel(tc, inputs, W, out):
    nc = tc.nc
    with ExitStack() as ctx:
        const = ctx.enter_context(tc.tile_pool(name="const", bufs=1))
        xpool = ctx.enter_context(tc.tile_pool(name="xpool", bufs=2))
        gpool = ctx.enter_context(tc.tile_pool(name="gpool", bufs=2))
        qpool = ctx.enter_context(tc.tile_pool(name="qpool", bufs=2))
        upool = ctx.enter_context(tc.tile_pool(name="upool", bufs=NG))
        wpool = ctx.enter_context(tc.tile_pool(name="wpool", bufs=4))
        cpool = ctx.enter_context(tc.tile_pool(name="cpool", bufs=3))
        opool = ctx.enter_context(tc.tile_pool(name="opool", bufs=2))
        small = ctx.enter_context(tc.tile_pool(name="small", bufs=NG + 1))
        psum_n = ctx.enter_context(tc.psum_pool(name="psum_n", bufs=1))
        psum_x = ctx.enter_context(tc.psum_pool(name="psum_x", bufs=4))
        psum_y = ctx.enter_context(tc.psum_pool(name="psum_y", bufs=3))
        if PIN:
            ctx.enter_context(tc.manual_schedule())

        ident = const.tile([P, P], F32, name="ident")
        masks.make_identity(nc, ident[:])
        m8 = const.tile([P, NCAP], F32, name="m8")
        nc.vector.tensor_reduce(
            out=m8[:], in_=ident[:].rearrange("p (n dl) -> p n dl", dl=DL), axis=AX.X, op=ALU.add
        )
        blk = const.tile([P, NCAP, DL], F32, name="blk")
        nc.vector.tensor_copy(out=blk[:], in_=m8[:].unsqueeze(2).to_broadcast([P, NCAP, DL]))
        neghalf = const.tile([P, GB], F32, name="neghalf")
        nc.vector.memset(neghalf[:], -0.5)
        zero = const.tile([P, 1], F32, name="zero")
        nc.vector.memset(zero[:], 0.0)
        epsc = const.tile([P, 1], F32, name="epsc")
        nc.vector.memset(epsc[:], EPS)
        ofin = const.tile([P, P], F32, name="ofin")
        nc.vector.memset(ofin[:], 0.0)
        junk = const.tile([P, S], F32, name="junk")
        junk_s = const.tile([P, S], F32, name="junk_s")

        xin = inputs.rearrange("(j p) b h -> p j b h", p=P)
        st = {}
        for q in range(NG):
            st[q] = {}

        def load(q):
            x = xpool.tile([P, SJ, GB, H], BF16, name="x")
            nc.sync.dma_start(out=x[:], in_=xin[:, :, q * GB : (q + 1) * GB, :])
            st[q]["x32"] = x[:].bitcast(F32)

        load(0)
        wraw = const.tile([P, 4, NCAP * DC], BF16, name="wraw")
        nc.sync.dma_start(
            out=wraw[:].rearrange("p (u e) c -> p u e c", u=2),
            in_=W[0].rearrange("(u p e) c -> p u e c", u=2, e=2),
        )
        load(1)
        loaded = [2]

        def load_up_to(n):
            while loaded[0] < min(n, NG):
                load(loaded[0])
                loaded[0] += 1

        wg = const.tile([P, DH, NCAP, DL, 4], BF16, name="wg", align_bytes=64)
        wview = wraw[:].rearrange("p t (n dh dl) -> p dh n dl t", dh=DH, dl=DL)
        for dh in range(DH):
            nc.vector.tensor_copy(out=wg[:, dh], in_=wview[:, dh])
        wq = const.tile([P, NCAP * DC], U32, name="wq", align_bytes=64)
        ws = const.tile([P, NCAP * DC], U8, name="ws", align_bytes=64)
        nc.vector.quantize_mx(
            out=wq[:].bitcast(FP8X4),
            scales=ws[:],
            in_=wg[:].rearrange("p dh n dl t -> p (dh n dl t)"),
        )

        def st_t(q, bl):
            s = st[q]
            tiles = []
            for half in range(2):
                xt = psum_y.tile([P, 2, 2, P], F32, name="xt", tag="Y")
                for jj in range(2):
                    for uu in range(2):
                        nc.tensor.transpose(
                            xt[:, jj, uu, :],
                            s["x32"][:, 2 * half + jj, bl, P * uu : P * uu + P],
                            ident[:],
                        )
                tiles.append(xt)
            s["xt", bl] = tiles

        def st_xc(q, bl):
            s = st[q]
            grouped = gpool.tile([P, 4 * S], BF16, name="grouped", align_bytes=64)
            g32 = grouped[:].bitcast(F32)
            for half in range(2):
                nc.scalar.copy(
                    out=g32[:, 512 * half : 512 * half + 512].rearrange(
                        "p (jj s uu) -> p jj s uu", jj=2, uu=2
                    ),
                    in_=s["xt", bl][half][:].rearrange("p jj uu s -> p jj s uu"),
                )
            s["grouped", bl] = grouped

        def st_q(q, bl):
            s = st[q]
            xq = qpool.tile([P, S], U32, name="xq", align_bytes=64)
            xs = qpool.tile([P, S], U8, name="xs", align_bytes=64)
            nc.vector.quantize_mx(
                out=xq[:].bitcast(FP8X4), scales=xs[:], in_=s["grouped", bl][:]
            )
            s["xq", bl] = (xq, xs)

        def st_mev(q, bl):
            s = st[q]
            xq, xs = s["xq", bl]
            if bl == 0:
                s["u"] = upool.tile([P, GB, DH, S], F32, name="u")
                s["v0s"] = small.tile([P, GB, DH], F32, name="v0s")
                s["v"] = small.tile([P, GB, DH], F32, name="v")
            for dh in range(DH):
                pb = psum_x.tile([P, S], F32, name="pb", tag="X")
                nc.tensor.matmul_mx(
                    out=pb[:],
                    lhsT=wq[:, P * dh : P * dh + P].bitcast(FP8X4),
                    lhsT_scale=ws[:, P * dh : P * dh + P],
                    rhs=xq[:].bitcast(FP8X4),
                    rhs_scale=xs[:],
                    start=True,
                    stop=True,
                )
                s["pb", bl, dh] = pb
                if dh in VECTOR_EVAC_DH:
                    nc.vector.tensor_scalar(
                        out=s["u"][:, bl, dh, :],
                        in0=s["pb", bl, dh][:],
                        scalar1=1.0,
                        scalar2=None,
                        op0=ALU.mult,
                        op1=ALU.add,
                        accum_out=s["v"][:, bl, dh : dh + 1],
                    )
                else:
                    nc.scalar.activation(
                        out=s["u"][:, bl, dh, :],
                        in_=s["pb", bl, dh][:],
                        func=ACT.Copy,
                        accum_out=s["v0s"][:, bl, dh : dh + 1],
                    )

        def st_v0(q):
            s = st[q]
            nc.vector.tensor_copy(
                out=s["v"][:].rearrange("p b (a e) -> p b a e", e=2)[:, :, :, 0],
                in_=s["v0s"][:].rearrange("p b (a e) -> p b a e", e=2)[:, :, :, 0],
            )

        def keep_clock(bank, passes):
            for i in range(passes):
                nc.tensor.matmul_mx(
                    out=bank[:].rearrange("p j c -> p (j c)"),
                    lhsT=wq[:, 0:P].bitcast(FP8X4),
                    lhsT_scale=ws[:, 0:P],
                    rhs=wq[:].bitcast(FP8X4),
                    rhs_scale=ws[:],
                    start=True,
                    stop=True,
                )

        def st_a1(q, r):
            s = st[q]
            pre = 1.0 / NCAP if r == 0 else 1.0
            sqj = small.tile([P, GB, DH], F32, name="sqj")
            ssq = small.tile([P, GB], F32, name="ssq")
            for bl in range(GB):
                nc.scalar.activation(
                    out=sqj[:, bl, :],
                    in_=s["v"][:, bl, :],
                    func=ACT.Square,
                    scale=pre,
                    accum_out=ssq[:, bl : bl + 1],
                )
            s["ssq"] = ssq

        def st_a2(q):
            s = st[q]
            n_ps = psum_n.tile([P, GB], F32, name="n_ps", tag="n")
            nc.tensor.matmul(
                out=n_ps[:],
                lhsT=blk[:].rearrange("p n dl -> p (n dl)"),
                rhs=s["ssq"][:],
                start=True,
                stop=True,
            )
            s["n_ps"] = n_ps

        def st_a3(q):
            s = st[q]
            xe = small.tile([P, GB], F32, name="xe")
            nc.scalar.activation(
                out=xe[:], in_=s["n_ps"][:], func=ACT.Identity, bias=epsc[:, 0:1]
            )
            s["xe"] = xe

        def st_a4(q):
            s = st[q]
            rs = small.tile([P, GB], F32, name="rs")
            nc.gpsimd.tensor_tensor(out=rs[:], in0=s["xe"][:], in1=neghalf[:], op=ALU.pow)
            s["rs"] = rs

        def st_a5(q, r):
            s = st[q]
            v = s["v"]
            rsb = s["rs"][:].unsqueeze(2).to_broadcast([P, GB, DH])
            if r == ROUNDS - 1:
                nc.gpsimd.tensor_tensor(
                    out=ofin[:, 0 : DH * B].rearrange("p (dh b) -> p b dh", dh=DH)[
                        :, q * GB : (q + 1) * GB, :
                    ],
                    in0=v[:],
                    in1=rsb,
                    op=ALU.mult,
                )
                return
            o = small.tile([P, GB, DH], F32, name="o")
            nc.gpsimd.tensor_tensor(out=o[:], in0=v[:], in1=rsb, op=ALU.mult)
            if r == 0:
                ocum = small.tile([P, GB, DH], F32, name="ocum")
                nc.gpsimd.tensor_scalar(
                    out=ocum[:], in0=o[:], scalar1=1.0 / NCAP, scalar2=0.0, op0=ALU.mult, op1=ALU.add
                )
                s["ocum"] = ocum
            else:
                nc.gpsimd.tensor_tensor(out=s["ocum"][:], in0=s["ocum"][:], in1=o[:], op=ALU.add)

        def st_b(q, r, bl):
            s = st[q]
            wt = wpool.tile([P, DH, S], F32, name="wt")
            for dh in range(DH):
                if dh in gpsimd_dh(r):
                    nc.gpsimd.tensor_scalar(
                        out=wt[:, dh, :],
                        in0=s["u"][:, bl, dh, :],
                        scalar1=s["ocum"][:, bl, dh : dh + 1],
                        scalar2=zero[:, 0:1],
                        op0=ALU.mult,
                        op1=ALU.add,
                    )
                else:
                    nc.scalar.activation(
                        out=wt[:, dh, :],
                        in_=s["u"][:, bl, dh, :],
                        func=ACT.Copy,
                        scale=s["ocum"][:, bl, dh : dh + 1],
                    )
            s["wt", bl] = wt

        def st_c(q, bl, passes):
            s = st[q]
            tp = psum_y.tile([P, SJ, P], F32, name="tp", tag="Y")
            keep_clock(tp, passes)
            for j in range(SJ):
                for dh in range(DH):
                    nc.tensor.matmul(
                        out=tp[:, j, :],
                        lhsT=s["wt", bl][:, dh, P * j : P * j + P],
                        rhs=ident[:],
                        is_transpose=True,
                        start=(dh == 0),
                        stop=(dh == DH - 1),
                    )
            s["tp", bl] = tp

        def st_d(q, bl):
            s = st[q]
            if bl == 0:
                s["t"] = small.tile([P, A, NCAP], F32, name="t")
            nc.vector.tensor_reduce(
                out=s["t"][:, bl * SJ : (bl + 1) * SJ, :],
                in_=s["tp", bl][:].rearrange("p j (n dl) -> p j n dl", dl=DL),
                axis=AX.X,
                op=ALU.add,
            )

        def st_e1(q):
            s = st[q]
            nmx = small.tile([P, A], F32, name="nmx")
            nc.vector.tensor_reduce(
                out=nmx[:], in_=s["t"][:], axis=AX.X, op=ALU.max, negate=True
            )
            s["nmx"] = nmx

        def st_e2(q):
            s = st[q]
            ex = small.tile([P, A, NCAP], F32, name="ex")
            sm = small.tile([P, A], F32, name="sm")
            for a in range(A):
                nc.scalar.activation(
                    out=ex[:, a, :],
                    in_=s["t"][:, a, :],
                    func=ACT.Exp,
                    bias=s["nmx"][:, a : a + 1],
                    accum_out=sm[:, a : a + 1],
                )
            s["ex"] = ex
            s["sm"] = sm

        def st_e3(q):
            s = st[q]
            rc = small.tile([P, A], F32, name="rc")
            nc.vector.reciprocal(out=rc[:], in_=s["sm"][:])
            s["rc"] = rc

        def st_e4(q, bl):
            s = st[q]
            crep = cpool.tile([P, SJ, NCAP, DL], F32, name="crep")
            for j in range(SJ):
                a = bl * SJ + j
                nc.scalar.activation(
                    out=crep[:, j],
                    in_=s["ex"][:, a, :].unsqueeze(2).to_broadcast([P, NCAP, DL]),
                    func=ACT.Copy,
                    scale=s["rc"][:, a : a + 1],
                )
            s["crep", bl] = crep

        def st_f(q):
            s = st[q]
            for bl in range(GB):
                s["cb", bl] = psum_x.tile([P, SJ, P], F32, name="cb", tag="X")
            keep_clock(s["cb", 0], 2)
            keep_clock(s["cb", 1], 1)
            for bl in range(GB):
                for j in range(SJ):
                    nc.tensor.transpose(
                        s["cb", bl][:, j, :],
                        s["crep", bl][:, j].rearrange("p n dl -> p (n dl)"),
                        ident[:],
                    )

        def st_g(q, bl):
            s = st[q]
            if bl == 0:
                s["vv"] = small.tile([P, GB, DH], F32, name="vv")
            for dh in range(DH - bl):
                nc.vector.scalar_tensor_tensor(
                    out=junk[:],
                    in0=s["u"][:, bl, dh, :],
                    scalar=1.0,
                    in1=s["cb", bl][:].rearrange("p j s -> p (j s)"),
                    op0=ALU.mult,
                    op1=ALU.mult,
                    accum_out=s["vv"][:, bl, dh : dh + 1],
                )

        def st_go12(q):
            s = st[q]
            cbs = opool.tile([P, S], F32, name="cbs")
            nc.scalar.copy(out=cbs[:], in_=s["cb", 1][:].rearrange("p j s -> p (j s)"))
            prod = opool.tile([P, S], F32, name="prod")
            nc.gpsimd.tensor_tensor(out=prod[:], in0=s["u"][:, 1, 3, :], in1=cbs[:], op=ALU.mult)
            s["prod"] = prod

        def st_go3(q):
            s = st[q]
            v = small.tile([P, GB, DH], F32, name="v")
            nc.scalar.activation(
                out=junk_s[:], in_=s["prod"][:], func=ACT.Copy, accum_out=v[:, 1, 3:4]
            )
            nc.scalar.copy(out=v[:, 0, :], in_=s["vv"][:, 0, :])
            nc.scalar.copy(out=v[:, 1, 0:3], in_=s["vv"][:, 1, 0:3])
            s["v"] = v

        def unit(k):
            return (k // NG, k % NG)

        def is_unit(k):
            return 0 <= k < NU

        def squashes(k):
            found = []
            if is_unit(k):
                found.append(unit(k))
            if 0 <= k - 1 - FINLAG < NG:
                found.append((ROUNDS - 1, k - 1 - FINLAG))
            return found

        def is_batch(b):
            return 0 <= b < B

        step = [-2]

        def proj_step():
            b = step[0]
            step[0] += 1
            if is_batch(b + 2) and (b + 2) % GB == 0:
                load_up_to((b + 2) // GB + 2)
            if is_batch(b + 1):
                st_q((b + 1) // GB, (b + 1) % GB)
            if is_batch(b):
                st_mev(b // GB, b % GB)
                if b % GB == GB - 1:
                    st_v0(b // GB)
            if is_batch(b + 2):
                st_t((b + 2) // GB, (b + 2) % GB)
                st_xc((b + 2) // GB, (b + 2) % GB)

        while step[0] < LEAD:
            proj_step()

        for t in range(-2, FINLAG + NG + 2):
            for r, q in squashes(t + 2):
                st_a1(q, r)
            if is_unit(t):
                r, q = unit(t)
                st_b(q, r, 0)
                st_b(q, r, 1)
            if is_unit(t - 4):
                st_go12(unit(t - 4)[1])
            if is_unit(t - 2):
                q = unit(t - 2)[1]
                st_d(q, 0)
                st_d(q, 1)
            for r, q in squashes(t + 1):
                st_a3(q)
                st_a4(q)
            proj_step()
            if is_unit(t - 1):
                q = unit(t - 1)[1]
                passes = 2 if step[0] >= B else 0
                st_c(q, 0, passes)
                st_c(q, 1, passes)
            if is_unit(t - 3):
                st_f(unit(t - 3)[1])
            if is_unit(t - 4):
                st_g(unit(t - 4)[1], 0)
            if is_unit(t - 2):
                q = unit(t - 2)[1]
                st_e1(q)
                st_e2(q)
            proj_step()
            if is_unit(t - 4):
                st_g(unit(t - 4)[1], 1)
            if is_unit(t - 2):
                q = unit(t - 2)[1]
                st_e3(q)
                st_e4(q, 0)
                st_e4(q, 1)
            if is_unit(t - 4):
                st_go3(unit(t - 4)[1])
            for r, q in squashes(t + 1):
                st_a5(q, r)
            for r, q in squashes(t + 2):
                st_a2(q)

        of_ps = psum_y.tile([P, P], F32, name="of_ps", tag="Y")
        nc.tensor.transpose(of_ps[:], ofin[:], ident[:])
        of_sb = const.tile([P, NCAP, DL], F32, name="of_sb")
        nc.vector.tensor_copy(out=of_sb[:].rearrange("p n dl -> p (n dl)"), in_=of_ps[:])
        for dh in range(DH):
            nc.sync.dma_start(
                out=out[:, :, DL * dh : DL * dh + DL], in_=of_sb[B * dh : B * dh + B, :, :]
            )
